import numpy as np
import ml_dtypes


def mxq(x, axis, fmt="e4m3"):
    dtype, down = {"e4m3": (ml_dtypes.float8_e4m3fn, 7), "e5m2": (ml_dtypes.float8_e5m2, 14)}[fmt]
    v = np.moveaxis(np.asarray(x, np.float32).astype(ml_dtypes.bfloat16).astype(np.float64), axis, -1)
    blocks = v.reshape(v.shape[:-1] + (-1, 32))
    amax = np.abs(blocks).max(-1, keepdims=True)
    byte = np.maximum(np.where(amax > 0, np.frexp(amax)[1] - 1 + 127, 0) - down, 1)
    scale = np.exp2(byte - 127.0)
    codes = (blocks / scale).astype(np.float32).astype(dtype).astype(np.float64)
    return np.moveaxis((codes * scale).reshape(v.shape), -1, axis)


WIDE = False


def mx_kscale(k):
    if not WIDE:
        return np.ones(k)
    levels = np.array([10, -10, 5, -5, 0])
    if k % 512:
        return np.exp2(np.random.permutation(np.resize(levels, k // 32))).repeat(32)
    a = np.empty((k // 512, 16))
    for p in range(k // 512):
        a[p, :8] = np.random.permutation(np.resize(levels, 8))
        for g in range(8):
            far = levels[np.abs(levels - a[p, g]) >= 10]
            a[p, g + 8] = far[np.random.randint(len(far))]
    return np.exp2(a.ravel()).repeat(32)


BF16 = ml_dtypes.bfloat16


def bf(x):
    return np.asarray(x, np.float32).astype(BF16)


def f64(x):
    return np.asarray(x).astype(np.float64)


B, D_IN, D_H, W_RANK, U_RANK = 1024, 1024, 2048, 512, 512


def sigmoid(v):
    return 1.0 / (1.0 + np.exp(-v))


def setup_inputs():
    s, t = mx_kscale(W_RANK), mx_kscale(U_RANK)
    return {
        "wx_r": bf(np.random.standard_normal((B, W_RANK)) * s),
        "uh_r": bf(np.random.standard_normal((B, U_RANK)) * t),
        "state": bf(np.random.standard_normal((B, D_H))),
        "W2": bf(np.random.standard_normal((D_H, W_RANK)) * 0.7 / np.sqrt(W_RANK) / s),
        "U2": bf(np.random.standard_normal((D_H, U_RANK)) * 0.7 / np.sqrt(U_RANK) / t),
        "bias_gate": bf(1.0 + 0.5 * np.random.standard_normal((1, D_H))),
        "bias_update": bf(1.0 + 0.5 * np.random.standard_normal((1, D_H))),
        "zeta": bf(1.0 + 0.1 * np.random.standard_normal((1, 1))),
        "nu": bf(-1.5 + 0.1 * np.random.standard_normal((1, 1))),
    }


def reference(wx_r, uh_r, state, W2, U2, bias_gate, bias_update, zeta, nu):
    wx = mxq(f64(wx_r), 1, "e4m3") @ mxq(f64(W2), 1, "e4m3").T
    uh = mxq(f64(uh_r), 1, "e4m3") @ mxq(f64(U2), 1, "e4m3").T
    pre = wx + uh
    z = sigmoid(pre + f64(bias_gate))
    h_cand = np.tanh(pre + f64(bias_update))
    return z * f64(state) + (sigmoid(f64(zeta)) * (1.0 - z) + sigmoid(f64(nu))) * h_cand

@@ -1,0 +1,254 @@
+from contextlib import ExitStack
+
+import concourse.mybir as mybir
+from concourse.masks import make_identity
+
+F32 = mybir.dt.float32
+BF16 = mybir.dt.bfloat16
+U32 = mybir.dt.uint32
+U8 = mybir.dt.uint8
+FP8X4 = mybir.dt.float8_e4m3fn_x4
+ACT = mybir.ActivationFunctionType
+ALU = mybir.AluOpType
+
+P = 128
+PACK = 4
+BATCH, HIDDEN, RANK = 1024, 2048, 512
+WORD_HALVES = 2
+STREAMS = 2
+ROWS_PER_PARTITION = BATCH // P
+HALF_CHUNKS = 4
+HALVES = ROWS_PER_PARTITION // HALF_CHUNKS
+HIDDEN_TILES = HIDDEN // P
+WEIGHT_LOAD_TILES = 2
+STATE_LOAD_TILES = 4
+UNITS = HIDDEN_TILES * HALVES
+TILES_AHEAD = 2
+OUT_LAG = 2
+
+FLOPS = 2 * BATCH * HIDDEN * RANK * STREAMS
+
+
+def tile_fastgrnncudacell_pa_kernel(
+    tc, wx_r, uh_r, state, W2, U2, bias_gate, bias_update, zeta, nu, out
+):
+    nc = tc.nc
+    assert tuple(wx_r.shape) == (BATCH, RANK) and tuple(W2.shape) == (HIDDEN, RANK)
+
+    act_views = [x.rearrange("(r i) k -> r i k", i=ROWS_PER_PARTITION) for x in (wx_r, uh_r)]
+    state_view = state.rearrange("(r i) d -> r i d", i=ROWS_PER_PARTITION)
+    out_view = out.rearrange("(r i) d -> r i d", i=ROWS_PER_PARTITION)
+    weight_views = [w.rearrange("(t m) k -> m t k", m=P) for w in (W2, U2)]
+
+    with ExitStack() as ctx:
+        ctx.enter_context(tc.manual_schedule())
+        keep = ctx.enter_context(tc.tile_pool(name="keep", bufs=1))
+        stage = ctx.enter_context(tc.tile_pool(name="stage", bufs=6))
+        gates_pool = ctx.enter_context(tc.tile_pool(name="gates", bufs=3))
+        mix_pool = ctx.enter_context(tc.tile_pool(name="mix", bufs=4))
+        out_pool = ctx.enter_context(tc.tile_pool(name="outs", bufs=6))
+        banks = ctx.enter_context(tc.psum_pool(name="banks", bufs=8))
+
+        identity = keep.tile([P, P], F32, name="identity")
+        make_identity(nc, identity[:])
+
+        bias_rows = keep.tile([P, P], BF16, name="bias_rows")
+        nc.vector.memset(bias_rows[:], 0.0)
+        for n, bias in enumerate((bias_gate, bias_update)):
+            nc.scalar.dma_start(
+                out=bias_rows[n * HIDDEN_TILES : (n + 1) * HIDDEN_TILES, :],
+                in_=bias.rearrange("o (t m) -> (o t) m", m=P),
+            )
+        zeta_col = keep.tile([P, 1], BF16, name="zeta_col")
+        nu_col = keep.tile([P, 1], BF16, name="nu_col")
+        nc.scalar.dma_start(out=zeta_col[:], in_=zeta.to_broadcast([P, 1]))
+        nc.scalar.dma_start(out=nu_col[:], in_=nu.to_broadcast([P, 1]))
+
+        act_raw = {}
+        weight_raw = {}
+        state_sb = {}
+
+        def load_acts(half):
+            for s in range(STREAMS):
+                raw = keep.tile([P, HALF_CHUNKS, RANK], BF16, name="act_raw_%d_%d" % (s, half))
+                chunks = slice(half * HALF_CHUNKS, (half + 1) * HALF_CHUNKS)
+                nc.sync.dma_start(out=raw[:], in_=act_views[s][:, chunks, :])
+                act_raw[(s, half)] = raw
+
+        def load_weights(n):
+            for s in range(STREAMS):
+                raw = keep.tile([P, WEIGHT_LOAD_TILES, RANK], BF16, name="weight_raw_%d_%d" % (s, n))
+                tiles = slice(n * WEIGHT_LOAD_TILES, (n + 1) * WEIGHT_LOAD_TILES)
+                nc.sync.dma_start(out=raw[:], in_=weight_views[s][:, tiles, :])
+                weight_raw[(s, n)] = raw
+
+        def load_state(n):
+            part = keep.tile([P, ROWS_PER_PARTITION, STATE_LOAD_TILES * P], BF16, name="state_%d" % n)
+            cols = slice(n * STATE_LOAD_TILES * P, (n + 1) * STATE_LOAD_TILES * P)
+            nc.sync.dma_start(out=part[:], in_=state_view[:, :, cols])
+            state_sb[n] = part
+
+        load_acts(0)
+        load_weights(0)
+        load_acts(1)
+        load_state(0)
+        load_weights(1)
+        for n in range(1, HIDDEN_TILES // STATE_LOAD_TILES):
+            load_weights(2 * n)
+            load_weights(2 * n + 1)
+            load_state(n)
+
+        sig_zeta = keep.tile([P, 1], F32, name="sig_zeta")
+        sig_nu = keep.tile([P, 1], F32, name="sig_nu")
+        nc.scalar.activation(out=sig_zeta[:], in_=zeta_col[:], func=ACT.Sigmoid)
+        nc.scalar.activation(out=sig_nu[:], in_=nu_col[:], func=ACT.Sigmoid)
+
+        act_codes = [keep.tile([P, BATCH], U32, name="act_codes_%d" % s, align_bytes=64) for s in range(STREAMS)]
+        act_scales = [keep.tile([P, BATCH], U8, name="act_scales_%d" % s, align_bytes=64) for s in range(STREAMS)]
+        weight_codes = keep.tile([P, STREAMS * HIDDEN], U32, name="weight_codes", align_bytes=64)
+        weight_scales = keep.tile([P, STREAMS * HIDDEN], U8, name="weight_scales", align_bytes=64)
+
+        def turn_rows(row_tiles, copy):
+            turned = banks.tile([P, WORD_HALVES, 2 * P], F32, tag="bank")
+            for n, rows in enumerate(row_tiles):
+                words = rows.bitcast(F32)
+                for h in range(WORD_HALVES):
+                    nc.tensor.transpose(
+                        turned[:, h, n * P : (n + 1) * P], words[:, h : WORD_HALVES * P : WORD_HALVES], identity[:]
+                    )
+            grouped = stage.tile([P, 2 * P, PACK], BF16, align_bytes=64)
+            copy(out=grouped[:].bitcast(F32), in_=turned[:].rearrange("p h r -> p r h"))
+            return grouped
+
+        def quantise(grouped, codes, scales):
+            nc.vector.quantize_mx(
+                out=codes.bitcast(FP8X4), scales=scales, in_=grouped[:].rearrange("p r t -> p (r t)")
+            )
+
+        def quantise_acts(half):
+            grouped = {}
+            for s, copy in enumerate((nc.vector.tensor_copy, nc.scalar.copy)):
+                for pair in range(HALF_CHUNKS // 2):
+                    raw = act_raw[(s, half)]
+                    grouped[(s, pair)] = turn_rows([raw[:, 2 * pair, :], raw[:, 2 * pair + 1, :]], copy)
+            for s in range(STREAMS):
+                for pair in range(HALF_CHUNKS // 2):
+                    first = (half * HALF_CHUNKS + 2 * pair) * P
+                    cols = slice(first, first + 2 * P)
+                    quantise(grouped[(s, pair)], act_codes[s][:, cols], act_scales[s][:, cols])
+
+        def turn_weights(t):
+            n, member = divmod(t, WEIGHT_LOAD_TILES)
+            return turn_rows([weight_raw[(s, n)][:, member, :] for s in range(STREAMS)], nc.scalar.copy)
+
+        def quantise_weights(t, grouped):
+            cols = slice(t * STREAMS * P, (t + 1) * STREAMS * P)
+            quantise(grouped, weight_codes[:, cols], weight_scales[:, cols])
+
+        pre = {}
+        cand = {}
+        gate = {}
+        cand_rows = {}
+        gate_rows = {}
+        drop = {}
+        gated = {}
+
+        def products(u):
+            t, half = divmod(u, HALVES)
+            pre[u] = banks.tile([P, HALF_CHUNKS * P], F32, name="pre", tag="bank")
+            b_cols = slice(half * HALF_CHUNKS * P, (half + 1) * HALF_CHUNKS * P)
+            for s in range(STREAMS):
+                w_cols = slice((t * STREAMS + s) * P, (t * STREAMS + s + 1) * P)
+                nc.tensor.matmul_mx(
+                    out=pre[u][:],
+                    lhsT=weight_codes[:, w_cols].bitcast(FP8X4),
+                    lhsT_scale=weight_scales[:, w_cols],
+                    rhs=act_codes[s][:, b_cols].bitcast(FP8X4),
+                    rhs_scale=act_scales[s][:, b_cols],
+                    start=(s == 0),
+                    stop=(s == STREAMS - 1),
+                )
+
+        def gates(u):
+            t = u // HALVES
+            cand[u] = gates_pool.tile([P, HALF_CHUNKS * P], F32, name="cand")
+            gate[u] = gates_pool.tile([P, HALF_CHUNKS * P], F32, name="gate")
+            nc.scalar.activation(
+                out=cand[u][:], in_=pre[u][:], func=ACT.Tanh,
+                bias=bias_cols[:, HIDDEN_TILES + t : HIDDEN_TILES + t + 1], scale=1.0,
+            )
+            nc.scalar.activation(
+                out=gate[u][:], in_=pre[u][:], func=ACT.Sigmoid, bias=bias_cols[:, t : t + 1], scale=1.0
+            )
+
+        def turn_back(u):
+            cand_rows[u] = banks.tile([P, HALF_CHUNKS, P], F32, name="cand_rows", tag="bank")
+            gate_rows[u] = banks.tile([P, HALF_CHUNKS, P], F32, name="gate_rows", tag="bank")
+            for turned, source in ((cand_rows[u], cand[u]), (gate_rows[u], gate[u])):
+                for i in range(HALF_CHUNKS):
+                    nc.tensor.transpose(turned[:, i, :], source[:, i * P : (i + 1) * P], identity[:])
+
+        def mix_drop(u):
+            t, half = divmod(u, HALVES)
+            n, member = divmod(t, STATE_LOAD_TILES)
+            chunks = slice(half * HALF_CHUNKS, (half + 1) * HALF_CHUNKS)
+            drop[u] = mix_pool.tile([P, HALF_CHUNKS, P], F32, name="drop")
+            nc.vector.scalar_tensor_tensor(
+                out=drop[u][:], in0=cand_rows[u][:], scalar=sig_zeta[:, 0:1],
+                in1=state_sb[n][:, chunks, member * P : (member + 1) * P],
+                op0=ALU.mult, op1=ALU.subtract,
+            )
+
+        def mix_gate(u):
+            gated[u] = mix_pool.tile([P, HALF_CHUNKS, P], F32, name="gated")
+            if u % HALVES == 0:
+                nc.vector.tensor_tensor(out=gated[u][:], in0=gate_rows[u][:], in1=drop[u][:], op=ALU.mult)
+            else:
+                z_rows = mix_pool.tile([P, HALF_CHUNKS, P], F32, name="z_rows")
+                nc.scalar.copy(out=z_rows[:], in_=gate_rows[u][:])
+                nc.gpsimd.tensor_tensor(out=gated[u][:], in0=z_rows[:], in1=drop[u][:], op=ALU.mult)
+
+        def mix_out(u):
+            t, half = divmod(u, HALVES)
+            chunks = slice(half * HALF_CHUNKS, (half + 1) * HALF_CHUNKS)
+            out_tile = out_pool.tile([P, HALF_CHUNKS, P], F32, name="out_tile")
+            nc.vector.scalar_tensor_tensor(
+                out=out_tile[:], in0=cand_rows[u][:], scalar=sig_sum[:, 0:1], in1=gated[u][:],
+                op0=ALU.mult, op1=ALU.subtract,
+            )
+            nc.sync.dma_start(out=out_view[:, chunks, t * P : (t + 1) * P], in_=out_tile[:])
+
+        quantise_acts(0)
+        quantise_weights(0, turn_weights(0))
+
+        bias_rows_f32 = keep.tile([P, P], F32, name="bias_rows_f32")
+        nc.vector.tensor_copy(out=bias_rows_f32[:], in_=bias_rows[:])
+        bias_turned = banks.tile([P, P], F32, tag="bank")
+        nc.tensor.transpose(bias_turned[:], bias_rows_f32[:], identity[:])
+        bias_cols = keep.tile([P, 2 * HIDDEN_TILES], F32, name="bias_cols")
+        nc.vector.tensor_copy(out=bias_cols[:], in_=bias_turned[:, 0 : 2 * HIDDEN_TILES])
+        sig_sum = keep.tile([P, 1], F32, name="sig_sum")
+        nc.vector.tensor_add(out=sig_sum[:], in0=sig_zeta[:], in1=sig_nu[:])
+
+        products(0)
+        gates(0)
+        quantise_acts(1)
+        quantise_weights(1, turn_weights(1))
+
+        grouped_ahead = {}
+        for u in range(UNITS + OUT_LAG):
+            t_ahead = u // HALVES + TILES_AHEAD
+            if u + 1 < UNITS:
+                products(u + 1)
+                gates(u + 1)
+            if u < UNITS:
+                turn_back(u)
+                if u % HALVES == 0 and t_ahead < HIDDEN_TILES:
+                    grouped_ahead[t_ahead] = turn_weights(t_ahead)
+                mix_drop(u)
+            if u >= OUT_LAG:
+                mix_out(u - OUT_LAG)
+            if u < UNITS:
+                mix_gate(u)
+                if u % HALVES == 1 and t_ahead < HIDDEN_TILES:
+                    quantise_weights(t_ahead, grouped_ahead[t_ahead])

@@ -14,17 +14,17 @@ ALU = mybir.AluOpType
 P = 128
 PACK = 4
 BATCH, HIDDEN, RANK = 1024, 2048, 512
-WORD_HALVES = 2
+WORD_SETS = 2
 STREAMS = 2
 ROWS_PER_PARTITION = BATCH // P
 HALF_CHUNKS = 4
 HALVES = ROWS_PER_PARTITION // HALF_CHUNKS
 HIDDEN_TILES = HIDDEN // P
-WEIGHT_LOAD_TILES = 2
-STATE_LOAD_TILES = 4
-UNITS = HIDDEN_TILES * HALVES
-TILES_AHEAD = 2
-OUT_LAG = 2
+GROUP = 2
+GROUPS = HIDDEN_TILES // GROUP
+BLOCK_TILES = 8
+BLOCKS = HIDDEN_TILES // BLOCK_TILES
+AHEAD = 3
 
 FLOPS = 2 * BATCH * HIDDEN * RANK * STREAMS
 
@@ -38,31 +38,23 @@ def tile_fastgrnncudacell_pa_kernel(
     act_views = [x.rearrange("(r i) k -> r i k", i=ROWS_PER_PARTITION) for x in (wx_r, uh_r)]
     state_view = state.rearrange("(r i) d -> r i d", i=ROWS_PER_PARTITION)
     out_view = out.rearrange("(r i) d -> r i d", i=ROWS_PER_PARTITION)
-    weight_views = [w.rearrange("(t m) k -> m t k", m=P) for w in (W2, U2)]
+    weight_views = [w.rearrange("(g m e) k -> g m e k", m=P, e=GROUP) for w in (W2, U2)]
+
+    units = [
+        (b * BLOCK_TILES + j, half)
+        for b in range(BLOCKS)
+        for half in range(HALVES)
+        for j in range(BLOCK_TILES)
+    ]
 
     with ExitStack() as ctx:
         ctx.enter_context(tc.manual_schedule())
         keep = ctx.enter_context(tc.tile_pool(name="keep", bufs=1))
         stage = ctx.enter_context(tc.tile_pool(name="stage", bufs=6))
-        gates_pool = ctx.enter_context(tc.tile_pool(name="gates", bufs=3))
-        mix_pool = ctx.enter_context(tc.tile_pool(name="mix", bufs=4))
-        out_pool = ctx.enter_context(tc.tile_pool(name="outs", bufs=6))
+        gates_pool = ctx.enter_context(tc.tile_pool(name="gates", bufs=5))
+        mix_pool = ctx.enter_context(tc.tile_pool(name="mix", bufs=3))
+        out_pool = ctx.enter_context(tc.tile_pool(name="outs", bufs=4))
         banks = ctx.enter_context(tc.psum_pool(name="banks", bufs=8))
-
-        identity = keep.tile([P, P], F32, name="identity")
-        make_identity(nc, identity[:])
-
-        bias_rows = keep.tile([P, P], BF16, name="bias_rows")
-        nc.vector.memset(bias_rows[:], 0.0)
-        for n, bias in enumerate((bias_gate, bias_update)):
-            nc.scalar.dma_start(
-                out=bias_rows[n * HIDDEN_TILES : (n + 1) * HIDDEN_TILES, :],
-                in_=bias.rearrange("o (t m) -> (o t) m", m=P),
-            )
-        zeta_col = keep.tile([P, 1], BF16, name="zeta_col")
-        nu_col = keep.tile([P, 1], BF16, name="nu_col")
-        nc.scalar.dma_start(out=zeta_col[:], in_=zeta.to_broadcast([P, 1]))
-        nc.scalar.dma_start(out=nu_col[:], in_=nu.to_broadcast([P, 1]))
 
         act_raw = {}
         weight_raw = {}
@@ -75,94 +67,121 @@ def tile_fastgrnncudacell_pa_kernel(
                 nc.sync.dma_start(out=raw[:], in_=act_views[s][:, chunks, :])
                 act_raw[(s, half)] = raw
 
-        def load_weights(n):
+        def load_weights(g):
             for s in range(STREAMS):
-                raw = keep.tile([P, WEIGHT_LOAD_TILES, RANK], BF16, name="weight_raw_%d_%d" % (s, n))
-                tiles = slice(n * WEIGHT_LOAD_TILES, (n + 1) * WEIGHT_LOAD_TILES)
-                nc.sync.dma_start(out=raw[:], in_=weight_views[s][:, tiles, :])
-                weight_raw[(s, n)] = raw
+                raw = keep.tile([P, GROUP, RANK], BF16, name="weight_raw_%d_%d" % (s, g))
+                nc.sync.dma_start(out=raw[:], in_=weight_views[s][g])
+                weight_raw[(s, g)] = raw
 
-        def load_state(n):
-            part = keep.tile([P, ROWS_PER_PARTITION, STATE_LOAD_TILES * P], BF16, name="state_%d" % n)
-            cols = slice(n * STATE_LOAD_TILES * P, (n + 1) * STATE_LOAD_TILES * P)
-            nc.sync.dma_start(out=part[:], in_=state_view[:, :, cols])
-            state_sb[n] = part
+        def load_state(b, half):
+            part = keep.tile([P, HALF_CHUNKS, BLOCK_TILES * P], BF16, name="state_%d_%d" % (b, half))
+            chunks = slice(half * HALF_CHUNKS, (half + 1) * HALF_CHUNKS)
+            cols = slice(b * BLOCK_TILES * P, (b + 1) * BLOCK_TILES * P)
+            nc.sync.dma_start(out=part[:], in_=state_view[:, chunks, cols])
+            state_sb[(b, half)] = part
 
         load_acts(0)
         load_weights(0)
-        load_acts(1)
-        load_state(0)
         load_weights(1)
-        for n in range(1, HIDDEN_TILES // STATE_LOAD_TILES):
-            load_weights(2 * n)
-            load_weights(2 * n + 1)
-            load_state(n)
+        load_weights(2)
+        load_state(0, 0)
+        load_weights(3)
+        load_acts(1)
+        load_state(0, 1)
+        load_weights(4)
+        load_weights(5)
+        load_state(1, 0)
+        load_weights(6)
+        load_weights(7)
+        load_state(1, 1)
 
-        sig_zeta = keep.tile([P, 1], F32, name="sig_zeta")
-        sig_nu = keep.tile([P, 1], F32, name="sig_nu")
-        nc.scalar.activation(out=sig_zeta[:], in_=zeta_col[:], func=ACT.Sigmoid)
-        nc.scalar.activation(out=sig_nu[:], in_=nu_col[:], func=ACT.Sigmoid)
+        bias_rows = keep.tile([P, P], BF16, name="bias_rows")
+        nc.vector.memset(bias_rows[:], 0.0)
+        zero_col = keep.tile([P, 1], F32, name="zero_col")
+        nc.vector.memset(zero_col[:], 0.0)
+        for n, bias in enumerate((bias_gate, bias_update)):
+            nc.scalar.dma_start(
+                out=bias_rows[n * HIDDEN_TILES : (n + 1) * HIDDEN_TILES, :],
+                in_=bias.rearrange("o (t m) -> (o t) m", m=P),
+            )
+        zeta_col = keep.tile([P, 1], BF16, name="zeta_col")
+        nu_col = keep.tile([P, 1], BF16, name="nu_col")
+        nc.scalar.dma_start(out=zeta_col[:], in_=zeta.to_broadcast([P, 1]))
+        nc.scalar.dma_start(out=nu_col[:], in_=nu.to_broadcast([P, 1]))
+
+        warm_col = keep.tile([P, 1], F32, name="warm_col")
+        nc.scalar.activation(out=warm_col[:], in_=zero_col[:], func=ACT.Sigmoid)
+
+        identity = keep.tile([P, P], F32, name="identity")
+        make_identity(nc, identity[:])
 
         act_codes = [keep.tile([P, BATCH], U32, name="act_codes_%d" % s, align_bytes=64) for s in range(STREAMS)]
         act_scales = [keep.tile([P, BATCH], U8, name="act_scales_%d" % s, align_bytes=64) for s in range(STREAMS)]
-        weight_codes = keep.tile([P, STREAMS * HIDDEN], U32, name="weight_codes", align_bytes=64)
-        weight_scales = keep.tile([P, STREAMS * HIDDEN], U8, name="weight_scales", align_bytes=64)
+        weight_codes = [keep.tile([P, HIDDEN], U32, name="weight_codes_%d" % s, align_bytes=64) for s in range(STREAMS)]
+        weight_scales = [keep.tile([P, HIDDEN], U8, name="weight_scales_%d" % s, align_bytes=64) for s in range(STREAMS)]
 
-        def turn_rows(row_tiles, copy):
-            turned = banks.tile([P, WORD_HALVES, 2 * P], F32, tag="bank")
+        def turn_rows(row_tiles):
+            turned = banks.tile([P, 2, WORD_SETS, P], F32, tag="bank")
             for n, rows in enumerate(row_tiles):
                 words = rows.bitcast(F32)
-                for h in range(WORD_HALVES):
-                    nc.tensor.transpose(
-                        turned[:, h, n * P : (n + 1) * P], words[:, h : WORD_HALVES * P : WORD_HALVES], identity[:]
-                    )
-            grouped = stage.tile([P, 2 * P, PACK], BF16, align_bytes=64)
-            copy(out=grouped[:].bitcast(F32), in_=turned[:].rearrange("p h r -> p r h"))
-            return grouped
+                for h in range(WORD_SETS):
+                    nc.tensor.transpose(turned[:, n, h, :], words[:, h : WORD_SETS * P : WORD_SETS], identity[:])
+            return turned
 
-        def quantise(grouped, codes, scales):
-            nc.vector.quantize_mx(
-                out=codes.bitcast(FP8X4), scales=scales, in_=grouped[:].rearrange("p r t -> p (r t)")
+        def act_job(s, half, pair):
+            first = (half * HALF_CHUNKS + 2 * pair) * P
+            cols = slice(first, first + 2 * P)
+            return {
+                "rows": [act_raw[(s, half)][:, 2 * pair + n, :] for n in range(2)],
+                "read": "p n h r -> p n r h", "write": "p (n r h) -> p n r h", "split": {"n": 2, "h": WORD_SETS},
+                "codes": act_codes[s][:, cols], "scales": act_scales[s][:, cols],
+            }
+
+        def weight_job(s, g):
+            cols = slice(g * GROUP * P, (g + 1) * GROUP * P)
+            return {
+                "rows": [weight_raw[(s, g)][:, e, :] for e in range(GROUP)],
+                "read": "p e h m -> p m e h", "write": "p (m e h) -> p m e h", "split": {"e": GROUP, "h": WORD_SETS},
+                "codes": weight_codes[s][:, cols], "scales": weight_scales[s][:, cols],
+            }
+
+        def job_turn(job):
+            job["turned"] = turn_rows(job["rows"])
+
+        def job_copy(job, copy):
+            grouped = stage.tile([P, 2 * P * PACK], BF16, name="grouped", align_bytes=64)
+            copy(
+                out=grouped[:].bitcast(F32).rearrange(job["write"], **job["split"]),
+                in_=job["turned"][:].rearrange(job["read"]),
             )
+            job["grouped"] = grouped
 
-        def quantise_acts(half):
-            grouped = {}
-            for s, copy in enumerate((nc.vector.tensor_copy, nc.scalar.copy)):
-                for pair in range(HALF_CHUNKS // 2):
-                    raw = act_raw[(s, half)]
-                    grouped[(s, pair)] = turn_rows([raw[:, 2 * pair, :], raw[:, 2 * pair + 1, :]], copy)
-            for s in range(STREAMS):
-                for pair in range(HALF_CHUNKS // 2):
-                    first = (half * HALF_CHUNKS + 2 * pair) * P
-                    cols = slice(first, first + 2 * P)
-                    quantise(grouped[(s, pair)], act_codes[s][:, cols], act_scales[s][:, cols])
-
-        def turn_weights(t):
-            n, member = divmod(t, WEIGHT_LOAD_TILES)
-            return turn_rows([weight_raw[(s, n)][:, member, :] for s in range(STREAMS)], nc.scalar.copy)
-
-        def quantise_weights(t, grouped):
-            cols = slice(t * STREAMS * P, (t + 1) * STREAMS * P)
-            quantise(grouped, weight_codes[:, cols], weight_scales[:, cols])
+        def job_quantise(job):
+            nc.vector.quantize_mx(out=job["codes"].bitcast(FP8X4), scales=job["scales"], in_=job["grouped"][:])
 
         pre = {}
         cand = {}
         gate = {}
-        cand_rows = {}
+        pull = {}
+        first_rows = {}
         gate_rows = {}
-        drop = {}
+        first = {}
         gated = {}
+        out_tiles = {}
+
+        def on_gpsimd(u):
+            return u % 3 != 0 and u < len(units) - 1
 
         def products(u):
-            t, half = divmod(u, HALVES)
+            t, half = units[u]
             pre[u] = banks.tile([P, HALF_CHUNKS * P], F32, name="pre", tag="bank")
             b_cols = slice(half * HALF_CHUNKS * P, (half + 1) * HALF_CHUNKS * P)
+            w_cols = slice(t * P, (t + 1) * P)
             for s in range(STREAMS):
-                w_cols = slice((t * STREAMS + s) * P, (t * STREAMS + s + 1) * P)
                 nc.tensor.matmul_mx(
                     out=pre[u][:],
-                    lhsT=weight_codes[:, w_cols].bitcast(FP8X4),
-                    lhsT_scale=weight_scales[:, w_cols],
+                    lhsT=weight_codes[s][:, w_cols].bitcast(FP8X4),
+                    lhsT_scale=weight_scales[s][:, w_cols],
                     rhs=act_codes[s][:, b_cols].bitcast(FP8X4),
                     rhs_scale=act_scales[s][:, b_cols],
                     start=(s == 0),
@@ -170,85 +189,144 @@ def tile_fastgrnncudacell_pa_kernel(
                 )
 
         def gates(u):
-            t = u // HALVES
-            cand[u] = gates_pool.tile([P, HALF_CHUNKS * P], F32, name="cand")
+            t, half = units[u]
             gate[u] = gates_pool.tile([P, HALF_CHUNKS * P], F32, name="gate")
+            cand[u] = gates_pool.tile([P, HALF_CHUNKS * P], F32, name="cand")
+            nc.scalar.activation(
+                out=gate[u][:], in_=pre[u][:], func=ACT.Sigmoid, bias=bias_cols[:, t : t + 1], scale=1.0
+            )
             nc.scalar.activation(
                 out=cand[u][:], in_=pre[u][:], func=ACT.Tanh,
                 bias=bias_cols[:, HIDDEN_TILES + t : HIDDEN_TILES + t + 1], scale=1.0,
             )
-            nc.scalar.activation(
-                out=gate[u][:], in_=pre[u][:], func=ACT.Sigmoid, bias=bias_cols[:, t : t + 1], scale=1.0
-            )
+            if on_gpsimd(u):
+                weight = gates_pool.tile([P, HALF_CHUNKS * P], F32, name="weight")
+                pull[u] = gates_pool.tile([P, HALF_CHUNKS * P], F32, name="pull")
+                nc.gpsimd.tensor_scalar(
+                    out=weight[:], in0=gate[u][:], scalar1=neg_zeta[:, 0:1], scalar2=sig_sum[:, 0:1],
+                    op0=ALU.mult, op1=ALU.add,
+                )
+                nc.gpsimd.tensor_tensor(out=pull[u][:], in0=weight[:], in1=cand[u][:], op=ALU.mult)
 
         def turn_back(u):
-            cand_rows[u] = banks.tile([P, HALF_CHUNKS, P], F32, name="cand_rows", tag="bank")
             gate_rows[u] = banks.tile([P, HALF_CHUNKS, P], F32, name="gate_rows", tag="bank")
-            for turned, source in ((cand_rows[u], cand[u]), (gate_rows[u], gate[u])):
+            first_rows[u] = banks.tile([P, HALF_CHUNKS, P], F32, name="first_rows", tag="bank")
+            turns = [(first_rows[u], cand[u]), (gate_rows[u], gate[u])]
+            if on_gpsimd(u):
+                turns = [(gate_rows[u], gate[u]), (first_rows[u], pull[u])]
+            for turned, source in turns:
                 for i in range(HALF_CHUNKS):
                     nc.tensor.transpose(turned[:, i, :], source[:, i * P : (i + 1) * P], identity[:])
 
-        def mix_drop(u):
-            t, half = divmod(u, HALVES)
-            n, member = divmod(t, STATE_LOAD_TILES)
-            chunks = slice(half * HALF_CHUNKS, (half + 1) * HALF_CHUNKS)
-            drop[u] = mix_pool.tile([P, HALF_CHUNKS, P], F32, name="drop")
-            nc.vector.scalar_tensor_tensor(
-                out=drop[u][:], in0=cand_rows[u][:], scalar=sig_zeta[:, 0:1],
-                in1=state_sb[n][:, chunks, member * P : (member + 1) * P],
-                op0=ALU.mult, op1=ALU.subtract,
-            )
+        def mix_first(u):
+            t, half = units[u]
+            b, member = divmod(t, BLOCK_TILES)
+            held = state_sb[(b, half)][:, :, member * P : (member + 1) * P]
+            first[u] = mix_pool.tile([P, HALF_CHUNKS, P], F32, name="first")
+            if on_gpsimd(u):
+                nc.vector.tensor_tensor(out=first[u][:], in0=gate_rows[u][:], in1=held, op=ALU.mult)
+            else:
+                nc.vector.scalar_tensor_tensor(
+                    out=first[u][:], in0=first_rows[u][:], scalar=sig_zeta[:, 0:1], in1=held,
+                    op0=ALU.mult, op1=ALU.subtract,
+                )
 
         def mix_gate(u):
-            gated[u] = mix_pool.tile([P, HALF_CHUNKS, P], F32, name="gated")
-            if u % HALVES == 0:
-                nc.vector.tensor_tensor(out=gated[u][:], in0=gate_rows[u][:], in1=drop[u][:], op=ALU.mult)
-            else:
-                z_rows = mix_pool.tile([P, HALF_CHUNKS, P], F32, name="z_rows")
-                nc.scalar.copy(out=z_rows[:], in_=gate_rows[u][:])
-                nc.gpsimd.tensor_tensor(out=gated[u][:], in0=z_rows[:], in1=drop[u][:], op=ALU.mult)
+            if not on_gpsimd(u):
+                gated[u] = mix_pool.tile([P, HALF_CHUNKS, P], F32, name="gated")
+                nc.vector.tensor_tensor(out=gated[u][:], in0=gate_rows[u][:], in1=first[u][:], op=ALU.mult)
 
         def mix_out(u):
-            t, half = divmod(u, HALVES)
+            t, half = units[u]
             chunks = slice(half * HALF_CHUNKS, (half + 1) * HALF_CHUNKS)
-            out_tile = out_pool.tile([P, HALF_CHUNKS, P], F32, name="out_tile")
-            nc.vector.scalar_tensor_tensor(
-                out=out_tile[:], in0=cand_rows[u][:], scalar=sig_sum[:, 0:1], in1=gated[u][:],
-                op0=ALU.mult, op1=ALU.subtract,
-            )
-            nc.sync.dma_start(out=out_view[:, chunks, t * P : (t + 1) * P], in_=out_tile[:])
+            g, member = divmod(t, GROUP)
+            if member == 0:
+                out_tiles[(g, half)] = out_pool.tile([P, HALF_CHUNKS, GROUP * P], F32, name="out_tile")
+            out_tile = out_tiles[(g, half)]
+            cols = slice(member * P, (member + 1) * P)
+            if on_gpsimd(u):
+                nc.vector.tensor_tensor(
+                    out=out_tile[:, :, cols], in0=first_rows[u][:], in1=first[u][:], op=ALU.add
+                )
+            else:
+                nc.vector.scalar_tensor_tensor(
+                    out=out_tile[:, :, cols], in0=first_rows[u][:], scalar=sig_sum[:, 0:1], in1=gated[u][:],
+                    op0=ALU.mult, op1=ALU.subtract,
+                )
+            if u >= len(units) - GROUP:
+                nc.sync.dma_start(out=out_view[:, chunks, t * P : (t + 1) * P], in_=out_tile[:, :, cols])
+            elif member == GROUP - 1:
+                nc.sync.dma_start(out=out_view[:, chunks, g * GROUP * P : (g + 1) * GROUP * P], in_=out_tile[:])
 
-        quantise_acts(0)
-        quantise_weights(0, turn_weights(0))
+        vector_copy, scalar_copy = nc.vector.tensor_copy, nc.scalar.copy
+        start_acts = [act_job(s, 0, pair) for s in range(STREAMS) for pair in range(HALF_CHUNKS // 2)]
+        start_weights = [weight_job(s, g) for g in range(3) for s in range(STREAMS)]
+
+        for n, job in enumerate(start_acts):
+            job_turn(job)
+            job_copy(job, vector_copy if n % 2 == 0 else scalar_copy)
+        job_quantise(start_acts[0])
+        job_quantise(start_acts[1])
 
         bias_rows_f32 = keep.tile([P, P], F32, name="bias_rows_f32")
         nc.vector.tensor_copy(out=bias_rows_f32[:], in_=bias_rows[:])
+        for job, copy in zip(start_weights[:2], (vector_copy, scalar_copy)):
+            job_turn(job)
+            job_copy(job, copy)
         bias_turned = banks.tile([P, P], F32, tag="bank")
         nc.tensor.transpose(bias_turned[:], bias_rows_f32[:], identity[:])
+        for job in start_acts[2:] + start_weights[:2]:
+            job_quantise(job)
         bias_cols = keep.tile([P, 2 * HIDDEN_TILES], F32, name="bias_cols")
         nc.vector.tensor_copy(out=bias_cols[:], in_=bias_turned[:, 0 : 2 * HIDDEN_TILES])
+
+        sig_zeta = keep.tile([P, 1], F32, name="sig_zeta")
+        sig_nu = keep.tile([P, 1], F32, name="sig_nu")
+        nc.scalar.activation(out=sig_zeta[:], in_=zeta_col[:], func=ACT.Sigmoid)
+        nc.scalar.activation(out=sig_nu[:], in_=nu_col[:], func=ACT.Sigmoid)
         sig_sum = keep.tile([P, 1], F32, name="sig_sum")
         nc.vector.tensor_add(out=sig_sum[:], in0=sig_zeta[:], in1=sig_nu[:])
+        neg_zeta = keep.tile([P, 1], F32, name="neg_zeta")
+        nc.vector.tensor_scalar_mul(neg_zeta[:], sig_zeta[:], -1.0)
 
-        products(0)
-        gates(0)
-        quantise_acts(1)
-        quantise_weights(1, turn_weights(1))
+        for job, copy in zip(start_weights[2:4], (vector_copy, scalar_copy)):
+            job_turn(job)
+            job_copy(job, copy)
+        for u in range(2):
+            products(u)
+            gates(u)
+        for job in start_weights[2:4]:
+            job_quantise(job)
+        for job in start_weights[4:]:
+            job_turn(job)
+            job_copy(job, vector_copy)
+        products(2)
+        gates(2)
+        for job in start_weights[4:]:
+            job_quantise(job)
 
-        grouped_ahead = {}
-        for u in range(UNITS + OUT_LAG):
-            t_ahead = u // HALVES + TILES_AHEAD
-            if u + 1 < UNITS:
-                products(u + 1)
-                gates(u + 1)
-            if u < UNITS:
+        urgent = [weight_job(s, 3) for s in range(STREAMS)]
+        urgent += [act_job(s, 1, pair) for s in range(STREAMS) for pair in range(HALF_CHUNKS // 2)]
+        later = [weight_job(s, g) for g in range(4, GROUPS) for s in range(STREAMS)]
+        jobs_at = {}
+        for n, job in enumerate(urgent):
+            jobs_at.setdefault(n // 2, []).append(job)
+        for n, job in enumerate(later):
+            jobs_at.setdefault(3 + 13 * n // (len(later) - 1), []).append(job)
+
+        for u in range(len(units) + 1):
+            if u + AHEAD < len(units):
+                products(u + AHEAD)
+                gates(u + AHEAD)
+            if u < len(units):
                 turn_back(u)
-                if u % HALVES == 0 and t_ahead < HIDDEN_TILES:
-                    grouped_ahead[t_ahead] = turn_weights(t_ahead)
-                mix_drop(u)
-            if u >= OUT_LAG:
-                mix_out(u - OUT_LAG)
-            if u < UNITS:
+                for job in jobs_at.get(u, []):
+                    job_turn(job)
+                    job_copy(job, scalar_copy)
+                mix_first(u)
+            if u > 0:
+                mix_out(u - 1)
+            if u < len(units):
                 mix_gate(u)
-                if u % HALVES == 1 and t_ahead < HIDDEN_TILES:
-                    quantise_weights(t_ahead, grouped_ahead[t_ahead])
+                for job in jobs_at.get(u - 1, []):
+                    job_quantise(job)

@@ -24,6 +24,8 @@ GROUP = 2
 GROUPS = HIDDEN_TILES // GROUP
 BLOCK_TILES = 8
 BLOCKS = HIDDEN_TILES // BLOCK_TILES
+STATE_TILES = 8
+STEP_UNITS = 1
 AHEAD = 3
 
 FLOPS = 2 * BATCH * HIDDEN * RANK * STREAMS
@@ -62,10 +64,11 @@ def tile_fastgrnncudacell_pa_kernel(
 
         def load_acts(half):
             for s in range(STREAMS):
-                raw = keep.tile([P, HALF_CHUNKS, RANK], BF16, name="act_raw_%d_%d" % (s, half))
-                chunks = slice(half * HALF_CHUNKS, (half + 1) * HALF_CHUNKS)
-                nc.sync.dma_start(out=raw[:], in_=act_views[s][:, chunks, :])
-                act_raw[(s, half)] = raw
+                for pair in range(HALF_CHUNKS // 2):
+                    raw = keep.tile([P, 2, RANK], BF16, name="act_raw_%d_%d_%d" % (s, half, pair))
+                    first = half * HALF_CHUNKS + 2 * pair
+                    nc.sync.dma_start(out=raw[:], in_=act_views[s][:, first : first + 2, :])
+                    act_raw[(s, half, pair)] = raw
 
         def load_weights(g):
             for s in range(STREAMS):
@@ -74,9 +77,9 @@ def tile_fastgrnncudacell_pa_kernel(
                 weight_raw[(s, g)] = raw
 
         def load_state(b, half):
-            part = keep.tile([P, HALF_CHUNKS, BLOCK_TILES * P], BF16, name="state_%d_%d" % (b, half))
+            part = keep.tile([P, HALF_CHUNKS, STATE_TILES * P], BF16, name="state_%d_%d" % (b, half))
             chunks = slice(half * HALF_CHUNKS, (half + 1) * HALF_CHUNKS)
-            cols = slice(b * BLOCK_TILES * P, (b + 1) * BLOCK_TILES * P)
+            cols = slice(b * STATE_TILES * P, (b + 1) * STATE_TILES * P)
             nc.sync.dma_start(out=part[:], in_=state_view[:, chunks, cols])
             state_sb[(b, half)] = part
 
@@ -84,8 +87,8 @@ def tile_fastgrnncudacell_pa_kernel(
         load_weights(0)
         load_weights(1)
         load_weights(2)
-        load_state(0, 0)
         load_weights(3)
+        load_state(0, 0)
         load_acts(1)
         load_state(0, 1)
         load_weights(4)
@@ -132,7 +135,7 @@ def tile_fastgrnncudacell_pa_kernel(
             first = (half * HALF_CHUNKS + 2 * pair) * P
             cols = slice(first, first + 2 * P)
             return {
-                "rows": [act_raw[(s, half)][:, 2 * pair + n, :] for n in range(2)],
+                "rows": [act_raw[(s, half, pair)][:, n, :] for n in range(2)],
                 "read": "p n h r -> p n r h", "write": "p (n r h) -> p n r h", "split": {"n": 2, "h": WORD_SETS},
                 "codes": act_codes[s][:, cols], "scales": act_scales[s][:, cols],
             }
@@ -159,6 +162,14 @@ def tile_fastgrnncudacell_pa_kernel(
         def job_quantise(job):
             nc.vector.quantize_mx(out=job["codes"].bitcast(FP8X4), scales=job["scales"], in_=job["grouped"][:])
 
+        act_jobs = [act_job(s, 1, pair) for s in range(STREAMS) for pair in range(HALF_CHUNKS // 2)]
+        weight_jobs = [weight_job(s, g) for g in range(4, GROUPS) for s in range(STREAMS)]
+        jobs_at = {}
+        for n, job in enumerate(act_jobs):
+            jobs_at.setdefault(n // 2 + 1, []).append(job)
+        for n, job in enumerate(weight_jobs):
+            jobs_at.setdefault(3 + 11 * n // (len(weight_jobs) - 1), []).append(job)
+
         pre = {}
         cand = {}
         gate = {}
@@ -170,7 +181,7 @@ def tile_fastgrnncudacell_pa_kernel(
         out_tiles = {}
 
         def on_gpsimd(u):
-            return u % 3 != 0 and u < len(units) - 1
+            return u % 3 != 0
 
         def products(u):
             t, half = units[u]
@@ -220,7 +231,7 @@ def tile_fastgrnncudacell_pa_kernel(
 
         def mix_first(u):
             t, half = units[u]
-            b, member = divmod(t, BLOCK_TILES)
+            b, member = divmod(t, STATE_TILES)
             held = state_sb[(b, half)][:, :, member * P : (member + 1) * P]
             first[u] = mix_pool.tile([P, HALF_CHUNKS, P], F32, name="first")
             if on_gpsimd(u):
@@ -240,39 +251,55 @@ def tile_fastgrnncudacell_pa_kernel(
             t, half = units[u]
             chunks = slice(half * HALF_CHUNKS, (half + 1) * HALF_CHUNKS)
             g, member = divmod(t, GROUP)
-            if member == 0:
-                out_tiles[(g, half)] = out_pool.tile([P, HALF_CHUNKS, GROUP * P], F32, name="out_tile")
+            alone = u >= len(units) - GROUP
+            if alone or member == 0:
+                width = P if alone else GROUP * P
+                out_tiles[(g, half)] = out_pool.tile([P, HALF_CHUNKS, width], F32, name="out_tile")
             out_tile = out_tiles[(g, half)]
-            cols = slice(member * P, (member + 1) * P)
-            if on_gpsimd(u):
-                nc.vector.tensor_tensor(
-                    out=out_tile[:, :, cols], in0=first_rows[u][:], in1=first[u][:], op=ALU.add
-                )
-            else:
-                nc.vector.scalar_tensor_tensor(
-                    out=out_tile[:, :, cols], in0=first_rows[u][:], scalar=sig_sum[:, 0:1], in1=gated[u][:],
-                    op0=ALU.mult, op1=ALU.subtract,
-                )
-            if u >= len(units) - GROUP:
-                nc.sync.dma_start(out=out_view[:, chunks, t * P : (t + 1) * P], in_=out_tile[:, :, cols])
-            elif member == GROUP - 1:
+            cols = slice(0, P) if alone else slice(member * P, (member + 1) * P)
+            pieces = 2 if u == len(units) - 1 else 1
+            for n in range(pieces):
+                part = slice(n * HALF_CHUNKS // pieces, (n + 1) * HALF_CHUNKS // pieces)
+                if on_gpsimd(u):
+                    nc.vector.tensor_tensor(
+                        out=out_tile[:, part, cols], in0=first_rows[u][:, part, :], in1=first[u][:, part, :],
+                        op=ALU.add,
+                    )
+                else:
+                    nc.vector.scalar_tensor_tensor(
+                        out=out_tile[:, part, cols], in0=first_rows[u][:, part, :], scalar=sig_sum[:, 0:1],
+                        in1=gated[u][:, part, :], op0=ALU.mult, op1=ALU.subtract,
+                    )
+                if pieces > 1:
+                    at = half * HALF_CHUNKS + part.start
+                    nc.sync.dma_start(
+                        out=out_view[:, at : at + HALF_CHUNKS // pieces, t * P : (t + 1) * P],
+                        in_=out_tile[:, part, cols],
+                    )
+            if alone and pieces == 1:
+                nc.sync.dma_start(out=out_view[:, chunks, t * P : (t + 1) * P], in_=out_tile[:])
+            elif member == GROUP - 1 and pieces == 1:
                 nc.sync.dma_start(out=out_view[:, chunks, g * GROUP * P : (g + 1) * GROUP * P], in_=out_tile[:])
 
-        vector_copy, scalar_copy = nc.vector.tensor_copy, nc.scalar.copy
+        vector_copy, scalar_copy, gpsimd_copy = nc.vector.tensor_copy, nc.scalar.copy, nc.gpsimd.tensor_copy
         start_acts = [act_job(s, 0, pair) for s in range(STREAMS) for pair in range(HALF_CHUNKS // 2)]
-        start_weights = [weight_job(s, g) for g in range(3) for s in range(STREAMS)]
+        start_weights = [weight_job(s, g) for g in range(4) for s in range(STREAMS)]
 
+        for n, job in enumerate(start_acts):
+            pass
         for n, job in enumerate(start_acts):
             job_turn(job)
             job_copy(job, vector_copy if n % 2 == 0 else scalar_copy)
+        for n, job in enumerate(start_weights[:2]):
+            pass
         job_quantise(start_acts[0])
         job_quantise(start_acts[1])
 
         bias_rows_f32 = keep.tile([P, P], F32, name="bias_rows_f32")
         nc.vector.tensor_copy(out=bias_rows_f32[:], in_=bias_rows[:])
-        for job, copy in zip(start_weights[:2], (vector_copy, scalar_copy)):
+        for n, job in enumerate(start_weights[:2]):
             job_turn(job)
-            job_copy(job, copy)
+            job_copy(job, vector_copy if n % 2 == 0 else scalar_copy)
         bias_turned = banks.tile([P, P], F32, tag="bank")
         nc.tensor.transpose(bias_turned[:], bias_rows_f32[:], identity[:])
         for job in start_acts[2:] + start_weights[:2]:
@@ -289,44 +316,53 @@ def tile_fastgrnncudacell_pa_kernel(
         neg_zeta = keep.tile([P, 1], F32, name="neg_zeta")
         nc.vector.tensor_scalar_mul(neg_zeta[:], sig_zeta[:], -1.0)
 
-        for job, copy in zip(start_weights[2:4], (vector_copy, scalar_copy)):
+        for n, job in enumerate(start_weights[2:4]):
+            pass
             job_turn(job)
-            job_copy(job, copy)
+            job_copy(job, vector_copy if n % 2 == 0 else scalar_copy)
         for u in range(2):
             products(u)
             gates(u)
         for job in start_weights[2:4]:
             job_quantise(job)
-        for job in start_weights[4:]:
+        for u in range(2, AHEAD):
+            more = start_weights[2 * u : 2 * u + 2]
+            for n, job in enumerate(more):
+                pass
+                job_turn(job)
+                job_copy(job, vector_copy)
+            products(u)
+            gates(u)
+            for job in more:
+                job_quantise(job)
+        rest = start_weights[2 * AHEAD :]
+        for n, job in enumerate(rest):
+            pass
             job_turn(job)
             job_copy(job, vector_copy)
-        products(2)
-        gates(2)
-        for job in start_weights[4:]:
+        for job in rest:
             job_quantise(job)
 
-        urgent = [weight_job(s, 3) for s in range(STREAMS)]
-        urgent += [act_job(s, 1, pair) for s in range(STREAMS) for pair in range(HALF_CHUNKS // 2)]
-        later = [weight_job(s, g) for g in range(4, GROUPS) for s in range(STREAMS)]
-        jobs_at = {}
-        for n, job in enumerate(urgent):
-            jobs_at.setdefault(n // 2, []).append(job)
-        for n, job in enumerate(later):
-            jobs_at.setdefault(3 + 13 * n // (len(later) - 1), []).append(job)
-
-        for u in range(len(units) + 1):
-            if u + AHEAD < len(units):
-                products(u + AHEAD)
-                gates(u + AHEAD)
-            if u < len(units):
+        for v in range(0, len(units) + STEP_UNITS, STEP_UNITS):
+            here = [u for u in range(v, v + STEP_UNITS) if u < len(units)]
+            for u in range(v + AHEAD, min(v + AHEAD + STEP_UNITS, len(units))):
+                products(u)
+                gates(u)
+            for u in here:
+                for job in jobs_at.get(u + 1, []):
+                    pass
+            for u in here:
                 turn_back(u)
+            for u in here:
                 for job in jobs_at.get(u, []):
                     job_turn(job)
                     job_copy(job, scalar_copy)
-                mix_first(u)
-            if u > 0:
-                mix_out(u - 1)
-            if u < len(units):
-                mix_gate(u)
+            for u in range(v, v + STEP_UNITS):
+                if u < len(units):
+                    mix_first(u)
+                if 0 < u <= len(units):
+                    mix_out(u - 1)
+                if u < len(units):
+                    mix_gate(u)
                 for job in jobs_at.get(u - 1, []):
                     job_quantise(job)

@@ -22,10 +22,10 @@ HALVES = ROWS_PER_PARTITION // HALF_CHUNKS
 HIDDEN_TILES = HIDDEN // P
 GROUP = 2
 GROUPS = HIDDEN_TILES // GROUP
-BLOCK_TILES = 8
+BLOCK_TILES = 16
 BLOCKS = HIDDEN_TILES // BLOCK_TILES
 STATE_TILES = 8
-STEP_UNITS = 1
+STEP_UNITS = 2
 AHEAD = 3
 
 FLOPS = 2 * BATCH * HIDDEN * RANK * STREAMS
@@ -53,7 +53,7 @@ def tile_fastgrnncudacell_pa_kernel(
         ctx.enter_context(tc.manual_schedule())
         keep = ctx.enter_context(tc.tile_pool(name="keep", bufs=1))
         stage = ctx.enter_context(tc.tile_pool(name="stage", bufs=6))
-        gates_pool = ctx.enter_context(tc.tile_pool(name="gates", bufs=5))
+        gates_pool = ctx.enter_context(tc.tile_pool(name="gates", bufs=6))
         mix_pool = ctx.enter_context(tc.tile_pool(name="mix", bufs=3))
         out_pool = ctx.enter_context(tc.tile_pool(name="outs", bufs=4))
         banks = ctx.enter_context(tc.psum_pool(name="banks", bufs=8))
@@ -89,13 +89,13 @@ def tile_fastgrnncudacell_pa_kernel(
         load_weights(2)
         load_weights(3)
         load_state(0, 0)
-        load_acts(1)
-        load_state(0, 1)
         load_weights(4)
         load_weights(5)
-        load_state(1, 0)
         load_weights(6)
         load_weights(7)
+        load_state(1, 0)
+        load_acts(1)
+        load_state(0, 1)
         load_state(1, 1)
 
         bias_rows = keep.tile([P, P], BF16, name="bias_rows")
@@ -163,12 +163,10 @@ def tile_fastgrnncudacell_pa_kernel(
             nc.vector.quantize_mx(out=job["codes"].bitcast(FP8X4), scales=job["scales"], in_=job["grouped"][:])
 
         act_jobs = [act_job(s, 1, pair) for s in range(STREAMS) for pair in range(HALF_CHUNKS // 2)]
-        weight_jobs = [weight_job(s, g) for g in range(4, GROUPS) for s in range(STREAMS)]
+        weight_jobs = [weight_job(s, g) for g in range(3, GROUPS) for s in range(STREAMS)]
         jobs_at = {}
-        for n, job in enumerate(act_jobs):
-            jobs_at.setdefault(n // 2 + 1, []).append(job)
-        for n, job in enumerate(weight_jobs):
-            jobs_at.setdefault(3 + 11 * n // (len(weight_jobs) - 1), []).append(job)
+        for n, job in enumerate(weight_jobs + act_jobs):
+            jobs_at.setdefault(n // 2 + 0, []).append(job)
 
         pre = {}
         cand = {}
@@ -181,7 +179,7 @@ def tile_fastgrnncudacell_pa_kernel(
         out_tiles = {}
 
         def on_gpsimd(u):
-            return u % 3 != 0
+            return u >= 8 and u % 4 != 0
 
         def products(u):
             t, half = units[u]
@@ -213,10 +211,16 @@ def tile_fastgrnncudacell_pa_kernel(
             if on_gpsimd(u):
                 weight = gates_pool.tile([P, HALF_CHUNKS * P], F32, name="weight")
                 pull[u] = gates_pool.tile([P, HALF_CHUNKS * P], F32, name="pull")
-                nc.gpsimd.tensor_scalar(
-                    out=weight[:], in0=gate[u][:], scalar1=neg_zeta[:, 0:1], scalar2=sig_sum[:, 0:1],
-                    op0=ALU.mult, op1=ALU.add,
-                )
+                if u % 2 == 0:
+                    nc.gpsimd.tensor_scalar(
+                        out=weight[:], in0=gate[u][:], scalar1=neg_zeta[:, 0:1], scalar2=sig_sum[:, 0:1],
+                        op0=ALU.mult, op1=ALU.add,
+                    )
+                else:
+                    nc.scalar.activation(
+                        out=weight[:], in_=gate[u][:], func=ACT.Identity,
+                        scale=neg_zeta[:, 0:1], bias=sig_sum[:, 0:1],
+                    )
                 nc.gpsimd.tensor_tensor(out=pull[u][:], in0=weight[:], in1=cand[u][:], op=ALU.mult)
 
         def turn_back(u):
@@ -283,7 +287,7 @@ def tile_fastgrnncudacell_pa_kernel(
 
         vector_copy, scalar_copy, gpsimd_copy = nc.vector.tensor_copy, nc.scalar.copy, nc.gpsimd.tensor_copy
         start_acts = [act_job(s, 0, pair) for s in range(STREAMS) for pair in range(HALF_CHUNKS // 2)]
-        start_weights = [weight_job(s, g) for g in range(4) for s in range(STREAMS)]
+        start_weights = [weight_job(s, g) for g in range(3) for s in range(STREAMS)]
 
         for n, job in enumerate(start_acts):
             pass

@@ -16,17 +16,22 @@ PACK = 4
 BATCH, HIDDEN, RANK = 1024, 2048, 512
 WORD_SETS = 2
 STREAMS = 2
+PAIR = 2
+COLS = PAIR * P
 ROWS_PER_PARTITION = BATCH // P
 HALF_CHUNKS = 4
+HALF_PAIRS = HALF_CHUNKS // PAIR
 HALVES = ROWS_PER_PARTITION // HALF_CHUNKS
+HALF_ROWS = HALF_CHUNKS * P
 HIDDEN_TILES = HIDDEN // P
-GROUP = 2
-GROUPS = HIDDEN_TILES // GROUP
-BLOCK_TILES = 16
-BLOCKS = HIDDEN_TILES // BLOCK_TILES
+GROUPS = HIDDEN_TILES // PAIR
 STATE_TILES = 8
-STEP_UNITS = 2
+STORE_TILES = 2
+UNITS = HIDDEN_TILES * HALVES
 AHEAD = 3
+STEP = 2
+HEAD_GROUPS = 4
+FIRST_SHARED = 7
 
 FLOPS = 2 * BATCH * HIDDEN * RANK * STREAMS
 
@@ -40,61 +45,52 @@ def tile_fastgrnncudacell_pa_kernel(
     act_views = [x.rearrange("(r i) k -> r i k", i=ROWS_PER_PARTITION) for x in (wx_r, uh_r)]
     state_view = state.rearrange("(r i) d -> r i d", i=ROWS_PER_PARTITION)
     out_view = out.rearrange("(r i) d -> r i d", i=ROWS_PER_PARTITION)
-    weight_views = [w.rearrange("(g m e) k -> g m e k", m=P, e=GROUP) for w in (W2, U2)]
-
-    units = [
-        (b * BLOCK_TILES + j, half)
-        for b in range(BLOCKS)
-        for half in range(HALVES)
-        for j in range(BLOCK_TILES)
-    ]
+    weight_views = [w.rearrange("(g m e) k -> g m e k", m=P, e=PAIR) for w in (W2, U2)]
 
     with ExitStack() as ctx:
         ctx.enter_context(tc.manual_schedule())
         keep = ctx.enter_context(tc.tile_pool(name="keep", bufs=1))
-        stage = ctx.enter_context(tc.tile_pool(name="stage", bufs=6))
+        stage = ctx.enter_context(tc.tile_pool(name="stage", bufs=4))
         gates_pool = ctx.enter_context(tc.tile_pool(name="gates", bufs=6))
         mix_pool = ctx.enter_context(tc.tile_pool(name="mix", bufs=3))
-        out_pool = ctx.enter_context(tc.tile_pool(name="outs", bufs=4))
+        out_pool = ctx.enter_context(tc.tile_pool(name="outs", bufs=5))
         banks = ctx.enter_context(tc.psum_pool(name="banks", bufs=8))
 
         act_raw = {}
         weight_raw = {}
         state_sb = {}
 
-        def load_acts(half):
+        def load_acts(half, pair):
+            first = half * HALF_CHUNKS + pair * PAIR
             for s in range(STREAMS):
-                for pair in range(HALF_CHUNKS // 2):
-                    raw = keep.tile([P, 2, RANK], BF16, name="act_raw_%d_%d_%d" % (s, half, pair))
-                    first = half * HALF_CHUNKS + 2 * pair
-                    nc.sync.dma_start(out=raw[:], in_=act_views[s][:, first : first + 2, :])
-                    act_raw[(s, half, pair)] = raw
+                raw = keep.tile([P, PAIR, RANK], BF16, name="act_raw_%d_%d_%d" % (s, half, pair))
+                nc.sync.dma_start(out=raw[:], in_=act_views[s][:, first : first + PAIR, :])
+                act_raw[(s, half, pair)] = raw
 
         def load_weights(g):
             for s in range(STREAMS):
-                raw = keep.tile([P, GROUP, RANK], BF16, name="weight_raw_%d_%d" % (s, g))
+                raw = keep.tile([P, PAIR, RANK], BF16, name="weight_raw_%d_%d" % (s, g))
                 nc.sync.dma_start(out=raw[:], in_=weight_views[s][g])
                 weight_raw[(s, g)] = raw
 
-        def load_state(b, half):
-            part = keep.tile([P, HALF_CHUNKS, STATE_TILES * P], BF16, name="state_%d_%d" % (b, half))
+        def load_state(n, half):
+            part = keep.tile([P, HALF_CHUNKS, STATE_TILES * P], BF16, name="state_%d_%d" % (n, half))
             chunks = slice(half * HALF_CHUNKS, (half + 1) * HALF_CHUNKS)
-            cols = slice(b * STATE_TILES * P, (b + 1) * STATE_TILES * P)
+            cols = slice(n * STATE_TILES * P, (n + 1) * STATE_TILES * P)
             nc.sync.dma_start(out=part[:], in_=state_view[:, chunks, cols])
-            state_sb[(b, half)] = part
+            state_sb[(n, half)] = part
 
-        load_acts(0)
+        load_acts(0, 0)
         load_weights(0)
-        load_weights(1)
-        load_weights(2)
-        load_weights(3)
+        load_acts(0, 1)
+        for g in range(1, 4):
+            load_weights(g)
         load_state(0, 0)
-        load_weights(4)
-        load_weights(5)
-        load_weights(6)
-        load_weights(7)
+        for g in range(4, GROUPS):
+            load_weights(g)
         load_state(1, 0)
-        load_acts(1)
+        for pair in range(HALF_PAIRS):
+            load_acts(1, pair)
         load_state(0, 1)
         load_state(1, 1)
 
@@ -117,256 +113,241 @@ def tile_fastgrnncudacell_pa_kernel(
 
         identity = keep.tile([P, P], F32, name="identity")
         make_identity(nc, identity[:])
+        bias_rows_f32 = keep.tile([P, P], F32, name="bias_rows_f32")
+        nc.gpsimd.tensor_copy(out=bias_rows_f32[:], in_=bias_rows[:])
 
-        act_codes = [keep.tile([P, BATCH], U32, name="act_codes_%d" % s, align_bytes=64) for s in range(STREAMS)]
-        act_scales = [keep.tile([P, BATCH], U8, name="act_scales_%d" % s, align_bytes=64) for s in range(STREAMS)]
-        weight_codes = [keep.tile([P, HIDDEN], U32, name="weight_codes_%d" % s, align_bytes=64) for s in range(STREAMS)]
-        weight_scales = [keep.tile([P, HIDDEN], U8, name="weight_scales_%d" % s, align_bytes=64) for s in range(STREAMS)]
+        act_codes = keep.tile([P, STREAMS * BATCH], U32, name="act_codes", align_bytes=64)
+        act_scales = keep.tile([P, STREAMS * BATCH], U8, name="act_scales", align_bytes=64)
+        weight_codes = keep.tile([P, STREAMS * HIDDEN], U32, name="weight_codes", align_bytes=64)
+        weight_scales = keep.tile([P, STREAMS * HIDDEN], U8, name="weight_scales", align_bytes=64)
 
-        def turn_rows(row_tiles):
-            turned = banks.tile([P, 2, WORD_SETS, P], F32, tag="bank")
-            for n, rows in enumerate(row_tiles):
-                words = rows.bitcast(F32)
+        def act_job(half, s, pairs):
+            first = s * BATCH + half * HALF_ROWS + pairs[0] * COLS
+            cols = slice(first, first + len(pairs) * COLS)
+            return {
+                "raws": [act_raw[(s, half, pair)] for pair in pairs],
+                "codes": act_codes[:, cols], "scales": act_scales[:, cols],
+                "read": "p n h r -> p n r h", "write": "p (n r h) -> p n r h",
+            }
+
+        def weight_job(g):
+            cols = slice(g * STREAMS * COLS, (g + 1) * STREAMS * COLS)
+            return {
+                "raws": [weight_raw[(s, g)] for s in range(STREAMS)],
+                "codes": weight_codes[:, cols], "scales": weight_scales[:, cols],
+                "read": "p n h r -> p r n h", "write": "p (r n h) -> p r n h",
+            }
+
+        def turn_part(job, part):
+            turned = banks.tile([P, PAIR, WORD_SETS, P], F32, name="turned", tag="bank")
+            for n in range(PAIR):
+                words = job["raws"][part][:, n, :].bitcast(F32)
                 for h in range(WORD_SETS):
                     nc.tensor.transpose(turned[:, n, h, :], words[:, h : WORD_SETS * P : WORD_SETS], identity[:])
             return turned
 
-        def act_job(s, half, pair):
-            first = (half * HALF_CHUNKS + 2 * pair) * P
-            cols = slice(first, first + 2 * P)
-            return {
-                "rows": [act_raw[(s, half, pair)][:, n, :] for n in range(2)],
-                "read": "p n h r -> p n r h", "write": "p (n r h) -> p n r h", "split": {"n": 2, "h": WORD_SETS},
-                "codes": act_codes[s][:, cols], "scales": act_scales[s][:, cols],
-            }
-
-        def weight_job(s, g):
-            cols = slice(g * GROUP * P, (g + 1) * GROUP * P)
-            return {
-                "rows": [weight_raw[(s, g)][:, e, :] for e in range(GROUP)],
-                "read": "p e h m -> p m e h", "write": "p (m e h) -> p m e h", "split": {"e": GROUP, "h": WORD_SETS},
-                "codes": weight_codes[s][:, cols], "scales": weight_scales[s][:, cols],
-            }
-
-        def job_turn(job):
-            job["turned"] = turn_rows(job["rows"])
-
-        def job_copy(job, copy):
-            grouped = stage.tile([P, 2 * P * PACK], BF16, name="grouped", align_bytes=64)
+        def copy_part(job, part, turned, copy):
+            if part == 0:
+                job["grouped"] = stage.tile([P, len(job["raws"]) * COLS * PACK], BF16, name="grouped", align_bytes=64)
+            span = slice(part * COLS * PACK, (part + 1) * COLS * PACK)
             copy(
-                out=grouped[:].bitcast(F32).rearrange(job["write"], **job["split"]),
-                in_=job["turned"][:].rearrange(job["read"]),
+                out=job["grouped"][:, span].bitcast(F32).rearrange(job["write"], n=PAIR, h=WORD_SETS),
+                in_=turned[:].rearrange(job["read"]),
             )
-            job["grouped"] = grouped
 
-        def job_quantise(job):
+        def quantise(job):
             nc.vector.quantize_mx(out=job["codes"].bitcast(FP8X4), scales=job["scales"], in_=job["grouped"][:])
-
-        act_jobs = [act_job(s, 1, pair) for s in range(STREAMS) for pair in range(HALF_CHUNKS // 2)]
-        weight_jobs = [weight_job(s, g) for g in range(3, GROUPS) for s in range(STREAMS)]
-        jobs_at = {}
-        for n, job in enumerate(weight_jobs + act_jobs):
-            jobs_at.setdefault(n // 2 + 0, []).append(job)
 
         pre = {}
         cand = {}
         gate = {}
         pull = {}
-        first_rows = {}
+        beside_rows = {}
         gate_rows = {}
         first = {}
         gated = {}
         out_tiles = {}
 
-        def on_gpsimd(u):
-            return u >= 8 and u % 4 != 0
+        def shared(u):
+            return u >= FIRST_SHARED and u % 4 != 0
 
-        def products(u):
-            t, half = units[u]
-            pre[u] = banks.tile([P, HALF_CHUNKS * P], F32, name="pre", tag="bank")
-            b_cols = slice(half * HALF_CHUNKS * P, (half + 1) * HALF_CHUNKS * P)
-            w_cols = slice(t * P, (t + 1) * P)
+        def products(u, pairs):
+            half, t = divmod(u, HIDDEN_TILES)
+            g, member = divmod(t, PAIR)
+            if pairs[0] == 0:
+                pre[u] = banks.tile([P, HALF_ROWS], F32, name="pre", tag="bank")
+            span = slice(pairs[0] * COLS, (pairs[-1] + 1) * COLS)
             for s in range(STREAMS):
+                w_first = (g * STREAMS + s) * COLS + member * P
+                w_cols = slice(w_first, w_first + P)
+                b_first = s * BATCH + half * HALF_ROWS
+                b_cols = slice(b_first + span.start, b_first + span.stop)
                 nc.tensor.matmul_mx(
-                    out=pre[u][:],
-                    lhsT=weight_codes[s][:, w_cols].bitcast(FP8X4),
-                    lhsT_scale=weight_scales[s][:, w_cols],
-                    rhs=act_codes[s][:, b_cols].bitcast(FP8X4),
-                    rhs_scale=act_scales[s][:, b_cols],
+                    out=pre[u][:, span],
+                    lhsT=weight_codes[:, w_cols].bitcast(FP8X4),
+                    lhsT_scale=weight_scales[:, w_cols],
+                    rhs=act_codes[:, b_cols].bitcast(FP8X4),
+                    rhs_scale=act_scales[:, b_cols],
                     start=(s == 0),
                     stop=(s == STREAMS - 1),
                 )
 
-        def gates(u):
-            t, half = units[u]
-            gate[u] = gates_pool.tile([P, HALF_CHUNKS * P], F32, name="gate")
-            cand[u] = gates_pool.tile([P, HALF_CHUNKS * P], F32, name="cand")
+        def gates(u, pairs):
+            t = u % HIDDEN_TILES
+            if pairs[0] == 0:
+                gate[u] = gates_pool.tile([P, HALF_ROWS], F32, name="gate")
+                cand[u] = gates_pool.tile([P, HALF_ROWS], F32, name="cand")
+            span = slice(pairs[0] * COLS, (pairs[-1] + 1) * COLS)
             nc.scalar.activation(
-                out=gate[u][:], in_=pre[u][:], func=ACT.Sigmoid, bias=bias_cols[:, t : t + 1], scale=1.0
+                out=gate[u][:, span], in_=pre[u][:, span], func=ACT.Sigmoid,
+                bias=bias_cols[:, t : t + 1], scale=1.0,
             )
             nc.scalar.activation(
-                out=cand[u][:], in_=pre[u][:], func=ACT.Tanh,
+                out=cand[u][:, span], in_=pre[u][:, span], func=ACT.Tanh,
                 bias=bias_cols[:, HIDDEN_TILES + t : HIDDEN_TILES + t + 1], scale=1.0,
             )
-            if on_gpsimd(u):
-                weight = gates_pool.tile([P, HALF_CHUNKS * P], F32, name="weight")
-                pull[u] = gates_pool.tile([P, HALF_CHUNKS * P], F32, name="pull")
-                if u % 2 == 0:
-                    nc.gpsimd.tensor_scalar(
-                        out=weight[:], in0=gate[u][:], scalar1=neg_zeta[:, 0:1], scalar2=sig_sum[:, 0:1],
-                        op0=ALU.mult, op1=ALU.add,
-                    )
-                else:
-                    nc.scalar.activation(
-                        out=weight[:], in_=gate[u][:], func=ACT.Identity,
-                        scale=neg_zeta[:, 0:1], bias=sig_sum[:, 0:1],
-                    )
-                nc.gpsimd.tensor_tensor(out=pull[u][:], in0=weight[:], in1=cand[u][:], op=ALU.mult)
+
+        def share(u):
+            weight = gates_pool.tile([P, HALF_ROWS], F32, name="weight")
+            pull[u] = gates_pool.tile([P, HALF_ROWS], F32, name="pull")
+            if u % 2 == 0:
+                nc.gpsimd.tensor_scalar(
+                    out=weight[:], in0=gate[u][:], scalar1=neg_zeta[:, 0:1], scalar2=sig_sum[:, 0:1],
+                    op0=ALU.mult, op1=ALU.add,
+                )
+            else:
+                nc.scalar.activation(
+                    out=weight[:], in_=gate[u][:], func=ACT.Identity, scale=neg_zeta[:, 0:1], bias=sig_sum[:, 0:1]
+                )
+            nc.gpsimd.tensor_tensor(out=pull[u][:], in0=weight[:], in1=cand[u][:], op=ALU.mult)
 
         def turn_back(u):
             gate_rows[u] = banks.tile([P, HALF_CHUNKS, P], F32, name="gate_rows", tag="bank")
-            first_rows[u] = banks.tile([P, HALF_CHUNKS, P], F32, name="first_rows", tag="bank")
-            turns = [(first_rows[u], cand[u]), (gate_rows[u], gate[u])]
-            if on_gpsimd(u):
-                turns = [(gate_rows[u], gate[u]), (first_rows[u], pull[u])]
+            beside_rows[u] = banks.tile([P, HALF_CHUNKS, P], F32, name="beside_rows", tag="bank")
+            turns = [(beside_rows[u], cand[u]), (gate_rows[u], gate[u])]
+            if shared(u):
+                turns = [(gate_rows[u], gate[u]), (beside_rows[u], pull[u])]
             for turned, source in turns:
                 for i in range(HALF_CHUNKS):
                     nc.tensor.transpose(turned[:, i, :], source[:, i * P : (i + 1) * P], identity[:])
 
         def mix_first(u):
-            t, half = units[u]
-            b, member = divmod(t, STATE_TILES)
-            held = state_sb[(b, half)][:, :, member * P : (member + 1) * P]
+            half, t = divmod(u, HIDDEN_TILES)
+            n, member = divmod(t, STATE_TILES)
+            held = state_sb[(n, half)][:, :, member * P : (member + 1) * P]
             first[u] = mix_pool.tile([P, HALF_CHUNKS, P], F32, name="first")
-            if on_gpsimd(u):
+            if shared(u):
                 nc.vector.tensor_tensor(out=first[u][:], in0=gate_rows[u][:], in1=held, op=ALU.mult)
             else:
                 nc.vector.scalar_tensor_tensor(
-                    out=first[u][:], in0=first_rows[u][:], scalar=sig_zeta[:, 0:1], in1=held,
+                    out=first[u][:], in0=beside_rows[u][:], scalar=sig_zeta[:, 0:1], in1=held,
                     op0=ALU.mult, op1=ALU.subtract,
                 )
 
         def mix_gate(u):
-            if not on_gpsimd(u):
+            if not shared(u):
                 gated[u] = mix_pool.tile([P, HALF_CHUNKS, P], F32, name="gated")
                 nc.vector.tensor_tensor(out=gated[u][:], in0=gate_rows[u][:], in1=first[u][:], op=ALU.mult)
 
         def mix_out(u):
-            t, half = units[u]
-            chunks = slice(half * HALF_CHUNKS, (half + 1) * HALF_CHUNKS)
-            g, member = divmod(t, GROUP)
-            alone = u >= len(units) - GROUP
-            if alone or member == 0:
-                width = P if alone else GROUP * P
-                out_tiles[(g, half)] = out_pool.tile([P, HALF_CHUNKS, width], F32, name="out_tile")
-            out_tile = out_tiles[(g, half)]
-            cols = slice(0, P) if alone else slice(member * P, (member + 1) * P)
-            pieces = 2 if u == len(units) - 1 else 1
+            half, t = divmod(u, HIDDEN_TILES)
+            alone = u >= UNITS - STORE_TILES
+            width = 1 if alone else STORE_TILES
+            member = t % width
+            if member == 0:
+                out_tiles[u - member] = out_pool.tile([P, HALF_CHUNKS, width * P], F32, name="out_tile")
+            out_tile = out_tiles[u - member]
+            cols = slice(member * P, (member + 1) * P)
+            pieces = 2 if u == UNITS - 1 else 1
             for n in range(pieces):
                 part = slice(n * HALF_CHUNKS // pieces, (n + 1) * HALF_CHUNKS // pieces)
-                if on_gpsimd(u):
+                if shared(u):
                     nc.vector.tensor_tensor(
-                        out=out_tile[:, part, cols], in0=first_rows[u][:, part, :], in1=first[u][:, part, :],
+                        out=out_tile[:, part, cols], in0=beside_rows[u][:, part, :], in1=first[u][:, part, :],
                         op=ALU.add,
                     )
                 else:
                     nc.vector.scalar_tensor_tensor(
-                        out=out_tile[:, part, cols], in0=first_rows[u][:, part, :], scalar=sig_sum[:, 0:1],
+                        out=out_tile[:, part, cols], in0=beside_rows[u][:, part, :], scalar=sig_sum[:, 0:1],
                         in1=gated[u][:, part, :], op0=ALU.mult, op1=ALU.subtract,
                     )
-                if pieces > 1:
-                    at = half * HALF_CHUNKS + part.start
-                    nc.sync.dma_start(
-                        out=out_view[:, at : at + HALF_CHUNKS // pieces, t * P : (t + 1) * P],
-                        in_=out_tile[:, part, cols],
-                    )
-            if alone and pieces == 1:
-                nc.sync.dma_start(out=out_view[:, chunks, t * P : (t + 1) * P], in_=out_tile[:])
-            elif member == GROUP - 1 and pieces == 1:
-                nc.sync.dma_start(out=out_view[:, chunks, g * GROUP * P : (g + 1) * GROUP * P], in_=out_tile[:])
+                if member == width - 1:
+                    chunks = slice(half * HALF_CHUNKS + part.start, half * HALF_CHUNKS + part.stop)
+                    d_cols = slice((t - member) * P, (t + 1) * P)
+                    nc.sync.dma_start(out=out_view[:, chunks, d_cols], in_=out_tile[:, part, :])
 
-        vector_copy, scalar_copy, gpsimd_copy = nc.vector.tensor_copy, nc.scalar.copy, nc.gpsimd.tensor_copy
-        start_acts = [act_job(s, 0, pair) for s in range(STREAMS) for pair in range(HALF_CHUNKS // 2)]
-        start_weights = [weight_job(s, g) for g in range(3) for s in range(STREAMS)]
+        vector_copy, scalar_copy = nc.vector.tensor_copy, nc.scalar.copy
+        both = list(range(HALF_PAIRS))
+        early_acts = [[act_job(0, s, [pair]) for s in range(STREAMS)] for pair in both]
+        weight_jobs = [weight_job(g) for g in range(GROUPS)]
 
-        for n, job in enumerate(start_acts):
-            pass
-        for n, job in enumerate(start_acts):
-            job_turn(job)
-            job_copy(job, vector_copy if n % 2 == 0 else scalar_copy)
-        for n, job in enumerate(start_weights[:2]):
-            pass
-        job_quantise(start_acts[0])
-        job_quantise(start_acts[1])
-
-        bias_rows_f32 = keep.tile([P, P], F32, name="bias_rows_f32")
-        nc.vector.tensor_copy(out=bias_rows_f32[:], in_=bias_rows[:])
-        for n, job in enumerate(start_weights[:2]):
-            job_turn(job)
-            job_copy(job, vector_copy if n % 2 == 0 else scalar_copy)
-        bias_turned = banks.tile([P, P], F32, tag="bank")
+        for job, copy in zip(early_acts[0], (vector_copy, scalar_copy)):
+            copy_part(job, 0, turn_part(job, 0), copy)
+        for s, copy in enumerate((vector_copy, scalar_copy)):
+            copy_part(weight_jobs[0], s, turn_part(weight_jobs[0], s), copy)
+        bias_turned = banks.tile([P, P], F32, name="bias_turned", tag="bank")
         nc.tensor.transpose(bias_turned[:], bias_rows_f32[:], identity[:])
-        for job in start_acts[2:] + start_weights[:2]:
-            job_quantise(job)
         bias_cols = keep.tile([P, 2 * HIDDEN_TILES], F32, name="bias_cols")
-        nc.vector.tensor_copy(out=bias_cols[:], in_=bias_turned[:, 0 : 2 * HIDDEN_TILES])
+        nc.scalar.copy(out=bias_cols[:], in_=bias_turned[:, 0 : 2 * HIDDEN_TILES])
+        for job in early_acts[0]:
+            quantise(job)
+        quantise(weight_jobs[0])
+        for job, copy in zip(early_acts[1], (vector_copy, scalar_copy)):
+            copy_part(job, 0, turn_part(job, 0), copy)
+        for u in range(2):
+            products(u, [0])
+            gates(u, [0])
+        for job in early_acts[1]:
+            quantise(job)
+        copy_part(weight_jobs[1], 0, turn_part(weight_jobs[1], 0), vector_copy)
+        for u in range(2):
+            products(u, [1])
+            gates(u, [1])
+        copy_part(weight_jobs[1], 1, turn_part(weight_jobs[1], 1), vector_copy)
+        quantise(weight_jobs[1])
 
         sig_zeta = keep.tile([P, 1], F32, name="sig_zeta")
         sig_nu = keep.tile([P, 1], F32, name="sig_nu")
         nc.scalar.activation(out=sig_zeta[:], in_=zeta_col[:], func=ACT.Sigmoid)
         nc.scalar.activation(out=sig_nu[:], in_=nu_col[:], func=ACT.Sigmoid)
         sig_sum = keep.tile([P, 1], F32, name="sig_sum")
-        nc.vector.tensor_add(out=sig_sum[:], in0=sig_zeta[:], in1=sig_nu[:])
+        nc.gpsimd.tensor_tensor(out=sig_sum[:], in0=sig_zeta[:], in1=sig_nu[:], op=ALU.add)
         neg_zeta = keep.tile([P, 1], F32, name="neg_zeta")
-        nc.vector.tensor_scalar_mul(neg_zeta[:], sig_zeta[:], -1.0)
+        nc.gpsimd.tensor_scalar(out=neg_zeta[:], in0=sig_zeta[:], scalar1=-1.0, scalar2=None, op0=ALU.mult)
 
-        for n, job in enumerate(start_weights[2:4]):
-            pass
-            job_turn(job)
-            job_copy(job, vector_copy if n % 2 == 0 else scalar_copy)
-        for u in range(2):
-            products(u)
-            gates(u)
-        for job in start_weights[2:4]:
-            job_quantise(job)
+        for g in range(2, HEAD_GROUPS):
+            copy_part(weight_jobs[g], 0, turn_part(weight_jobs[g], 0), vector_copy)
+            copy_part(weight_jobs[g], 1, turn_part(weight_jobs[g], 1), scalar_copy)
+            quantise(weight_jobs[g])
         for u in range(2, AHEAD):
-            more = start_weights[2 * u : 2 * u + 2]
-            for n, job in enumerate(more):
-                pass
-                job_turn(job)
-                job_copy(job, vector_copy)
-            products(u)
-            gates(u)
-            for job in more:
-                job_quantise(job)
-        rest = start_weights[2 * AHEAD :]
-        for n, job in enumerate(rest):
-            pass
-            job_turn(job)
-            job_copy(job, vector_copy)
-        for job in rest:
-            job_quantise(job)
+            products(u, both)
+            gates(u, both)
+            if shared(u):
+                share(u)
 
-        for v in range(0, len(units) + STEP_UNITS, STEP_UNITS):
-            here = [u for u in range(v, v + STEP_UNITS) if u < len(units)]
-            for u in range(v + AHEAD, min(v + AHEAD + STEP_UNITS, len(units))):
-                products(u)
-                gates(u)
-            for u in here:
-                for job in jobs_at.get(u + 1, []):
-                    pass
-            for u in here:
+        jobs = weight_jobs[HEAD_GROUPS:] + [act_job(1, s, both) for s in range(STREAMS)]
+        jobs_at = {}
+        for n, job in enumerate(jobs):
+            jobs_at.setdefault(n, []).append(job)
+
+        for v in range(0, UNITS + STEP, STEP):
+            for u in range(v + AHEAD, min(v + AHEAD + STEP, UNITS)):
+                products(u, both)
+                gates(u, both)
+                if shared(u):
+                    share(u)
+            for u in range(v, min(v + STEP, UNITS)):
                 turn_back(u)
-            for u in here:
+            for u in range(v, min(v + STEP, UNITS)):
                 for job in jobs_at.get(u, []):
-                    job_turn(job)
-                    job_copy(job, scalar_copy)
-            for u in range(v, v + STEP_UNITS):
-                if u < len(units):
+                    for part in range(len(job["raws"])):
+                        copy_part(job, part, turn_part(job, part), scalar_copy)
+            for u in range(v, v + STEP):
+                if u < UNITS:
                     mix_first(u)
-                if 0 < u <= len(units):
+                if 0 < u <= UNITS:
                     mix_out(u - 1)
-                if u < len(units):
+                if u < UNITS:
                     mix_gate(u)
                 for job in jobs_at.get(u - 1, []):
-                    job_quantise(job)
+                    quantise(job)

from contextlib import ExitStack

import concourse.mybir as mybir
from concourse.masks import make_identity

F32 = mybir.dt.float32
BF16 = mybir.dt.bfloat16
U32 = mybir.dt.uint32
U8 = mybir.dt.uint8
FP8X4 = mybir.dt.float8_e4m3fn_x4
ACT = mybir.ActivationFunctionType
ALU = mybir.AluOpType

P = 128
PACK = 4
BATCH, HIDDEN, RANK = 1024, 2048, 512
WORD_SETS = 2
STREAMS = 2
PAIR = 2
COLS = PAIR * P
ROWS_PER_PARTITION = BATCH // P
HALF_CHUNKS = 4
HALF_PAIRS = HALF_CHUNKS // PAIR
HALVES = ROWS_PER_PARTITION // HALF_CHUNKS
HALF_ROWS = HALF_CHUNKS * P
HIDDEN_TILES = HIDDEN // P
GROUPS = HIDDEN_TILES // PAIR
STATE_TILES = 8
STORE_TILES = 2
UNITS = HIDDEN_TILES * HALVES
AHEAD = 3
STEP = 2
HEAD_GROUPS = 4
FIRST_SHARED = 7

FLOPS = 2 * BATCH * HIDDEN * RANK * STREAMS


def tile_fastgrnncudacell_pa_kernel(
    tc, wx_r, uh_r, state, W2, U2, bias_gate, bias_update, zeta, nu, out
):
    nc = tc.nc
    assert tuple(wx_r.shape) == (BATCH, RANK) and tuple(W2.shape) == (HIDDEN, RANK)

    act_views = [x.rearrange("(r i) k -> r i k", i=ROWS_PER_PARTITION) for x in (wx_r, uh_r)]
    state_view = state.rearrange("(r i) d -> r i d", i=ROWS_PER_PARTITION)
    out_view = out.rearrange("(r i) d -> r i d", i=ROWS_PER_PARTITION)
    weight_views = [w.rearrange("(g m e) k -> g m e k", m=P, e=PAIR) for w in (W2, U2)]

    with ExitStack() as ctx:
        ctx.enter_context(tc.manual_schedule())
        keep = ctx.enter_context(tc.tile_pool(name="keep", bufs=1))
        stage = ctx.enter_context(tc.tile_pool(name="stage", bufs=4))
        gates_pool = ctx.enter_context(tc.tile_pool(name="gates", bufs=6))
        mix_pool = ctx.enter_context(tc.tile_pool(name="mix", bufs=3))
        out_pool = ctx.enter_context(tc.tile_pool(name="outs", bufs=5))
        banks = ctx.enter_context(tc.psum_pool(name="banks", bufs=8))

        act_raw = {}
        weight_raw = {}
        state_sb = {}

        def load_acts(half, pair):
            first = half * HALF_CHUNKS + pair * PAIR
            for s in range(STREAMS):
                raw = keep.tile([P, PAIR, RANK], BF16, name="act_raw_%d_%d_%d" % (s, half, pair))
                nc.sync.dma_start(out=raw[:], in_=act_views[s][:, first : first + PAIR, :])
                act_raw[(s, half, pair)] = raw

        def load_weights(g):
            for s in range(STREAMS):
                raw = keep.tile([P, PAIR, RANK], BF16, name="weight_raw_%d_%d" % (s, g))
                nc.sync.dma_start(out=raw[:], in_=weight_views[s][g])
                weight_raw[(s, g)] = raw

        def load_state(n, half):
            part = keep.tile([P, HALF_CHUNKS, STATE_TILES * P], BF16, name="state_%d_%d" % (n, half))
            chunks = slice(half * HALF_CHUNKS, (half + 1) * HALF_CHUNKS)
            cols = slice(n * STATE_TILES * P, (n + 1) * STATE_TILES * P)
            nc.sync.dma_start(out=part[:], in_=state_view[:, chunks, cols])
            state_sb[(n, half)] = part

        load_acts(0, 0)
        load_weights(0)
        load_acts(0, 1)
        for g in range(1, 4):
            load_weights(g)
        load_state(0, 0)
        for g in range(4, GROUPS):
            load_weights(g)
        load_state(1, 0)
        for pair in range(HALF_PAIRS):
            load_acts(1, pair)
        load_state(0, 1)
        load_state(1, 1)

        bias_rows = keep.tile([P, P], BF16, name="bias_rows")
        nc.vector.memset(bias_rows[:], 0.0)
        zero_col = keep.tile([P, 1], F32, name="zero_col")
        nc.vector.memset(zero_col[:], 0.0)
        for n, bias in enumerate((bias_gate, bias_update)):
            nc.scalar.dma_start(
                out=bias_rows[n * HIDDEN_TILES : (n + 1) * HIDDEN_TILES, :],
                in_=bias.rearrange("o (t m) -> (o t) m", m=P),
            )
        zeta_col = keep.tile([P, 1], BF16, name="zeta_col")
        nu_col = keep.tile([P, 1], BF16, name="nu_col")
        nc.scalar.dma_start(out=zeta_col[:], in_=zeta.to_broadcast([P, 1]))
        nc.scalar.dma_start(out=nu_col[:], in_=nu.to_broadcast([P, 1]))

        warm_col = keep.tile([P, 1], F32, name="warm_col")
        nc.scalar.activation(out=warm_col[:], in_=zero_col[:], func=ACT.Sigmoid)

        identity = keep.tile([P, P], F32, name="identity")
        make_identity(nc, identity[:])
        bias_rows_f32 = keep.tile([P, P], F32, name="bias_rows_f32")
        nc.gpsimd.tensor_copy(out=bias_rows_f32[:], in_=bias_rows[:])

        act_codes = keep.tile([P, STREAMS * BATCH], U32, name="act_codes", align_bytes=64)
        act_scales = keep.tile([P, STREAMS * BATCH], U8, name="act_scales", align_bytes=64)
        weight_codes = keep.tile([P, STREAMS * HIDDEN], U32, name="weight_codes", align_bytes=64)
        weight_scales = keep.tile([P, STREAMS * HIDDEN], U8, name="weight_scales", align_bytes=64)

        def act_job(half, s, pairs):
            first = s * BATCH + half * HALF_ROWS + pairs[0] * COLS
            cols = slice(first, first + len(pairs) * COLS)
            return {
                "raws": [act_raw[(s, half, pair)] for pair in pairs],
                "codes": act_codes[:, cols], "scales": act_scales[:, cols],
                "read": "p n h r -> p n r h", "write": "p (n r h) -> p n r h",
            }

        def weight_job(g):
            cols = slice(g * STREAMS * COLS, (g + 1) * STREAMS * COLS)
            return {
                "raws": [weight_raw[(s, g)] for s in range(STREAMS)],
                "codes": weight_codes[:, cols], "scales": weight_scales[:, cols],
                "read": "p n h r -> p r n h", "write": "p (r n h) -> p r n h",
            }

        def turn_part(job, part):
            turned = banks.tile([P, PAIR, WORD_SETS, P], F32, name="turned", tag="bank")
            for n in range(PAIR):
                words = job["raws"][part][:, n, :].bitcast(F32)
                for h in range(WORD_SETS):
                    nc.tensor.transpose(turned[:, n, h, :], words[:, h : WORD_SETS * P : WORD_SETS], identity[:])
            return turned

        def copy_part(job, part, turned, copy):
            if part == 0:
                job["grouped"] = stage.tile([P, len(job["raws"]) * COLS * PACK], BF16, name="grouped", align_bytes=64)
            span = slice(part * COLS * PACK, (part + 1) * COLS * PACK)
            copy(
                out=job["grouped"][:, span].bitcast(F32).rearrange(job["write"], n=PAIR, h=WORD_SETS),
                in_=turned[:].rearrange(job["read"]),
            )

        def quantise(job):
            nc.vector.quantize_mx(out=job["codes"].bitcast(FP8X4), scales=job["scales"], in_=job["grouped"][:])

        pre = {}
        cand = {}
        gate = {}
        pull = {}
        beside_rows = {}
        gate_rows = {}
        first = {}
        gated = {}
        out_tiles = {}

        def shared(u):
            return u >= FIRST_SHARED and u % 4 != 0

        def products(u, pairs):
            half, t = divmod(u, HIDDEN_TILES)
            g, member = divmod(t, PAIR)
            if pairs[0] == 0:
                pre[u] = banks.tile([P, HALF_ROWS], F32, name="pre", tag="bank")
            span = slice(pairs[0] * COLS, (pairs[-1] + 1) * COLS)
            for s in range(STREAMS):
                w_first = (g * STREAMS + s) * COLS + member * P
                w_cols = slice(w_first, w_first + P)
                b_first = s * BATCH + half * HALF_ROWS
                b_cols = slice(b_first + span.start, b_first + span.stop)
                nc.tensor.matmul_mx(
                    out=pre[u][:, span],
                    lhsT=weight_codes[:, w_cols].bitcast(FP8X4),
                    lhsT_scale=weight_scales[:, w_cols],
                    rhs=act_codes[:, b_cols].bitcast(FP8X4),
                    rhs_scale=act_scales[:, b_cols],
                    start=(s == 0),
                    stop=(s == STREAMS - 1),
                )

        def gates(u, pairs):
            t = u % HIDDEN_TILES
            if pairs[0] == 0:
                gate[u] = gates_pool.tile([P, HALF_ROWS], F32, name="gate")
                cand[u] = gates_pool.tile([P, HALF_ROWS], F32, name="cand")
            span = slice(pairs[0] * COLS, (pairs[-1] + 1) * COLS)
            nc.scalar.activation(
                out=gate[u][:, span], in_=pre[u][:, span], func=ACT.Sigmoid,
                bias=bias_cols[:, t : t + 1], scale=1.0,
            )
            nc.scalar.activation(
                out=cand[u][:, span], in_=pre[u][:, span], func=ACT.Tanh,
                bias=bias_cols[:, HIDDEN_TILES + t : HIDDEN_TILES + t + 1], scale=1.0,
            )

        def share(u):
            weight = gates_pool.tile([P, HALF_ROWS], F32, name="weight")
            pull[u] = gates_pool.tile([P, HALF_ROWS], F32, name="pull")
            if u % 2 == 0:
                nc.gpsimd.tensor_scalar(
                    out=weight[:], in0=gate[u][:], scalar1=neg_zeta[:, 0:1], scalar2=sig_sum[:, 0:1],
                    op0=ALU.mult, op1=ALU.add,
                )
            else:
                nc.scalar.activation(
                    out=weight[:], in_=gate[u][:], func=ACT.Identity, scale=neg_zeta[:, 0:1], bias=sig_sum[:, 0:1]
                )
            nc.gpsimd.tensor_tensor(out=pull[u][:], in0=weight[:], in1=cand[u][:], op=ALU.mult)

        def turn_back(u):
            gate_rows[u] = banks.tile([P, HALF_CHUNKS, P], F32, name="gate_rows", tag="bank")
            beside_rows[u] = banks.tile([P, HALF_CHUNKS, P], F32, name="beside_rows", tag="bank")
            turns = [(beside_rows[u], cand[u]), (gate_rows[u], gate[u])]
            if shared(u):
                turns = [(gate_rows[u], gate[u]), (beside_rows[u], pull[u])]
            for turned, source in turns:
                for i in range(HALF_CHUNKS):
                    nc.tensor.transpose(turned[:, i, :], source[:, i * P : (i + 1) * P], identity[:])

        def mix_first(u):
            half, t = divmod(u, HIDDEN_TILES)
            n, member = divmod(t, STATE_TILES)
            held = state_sb[(n, half)][:, :, member * P : (member + 1) * P]
            first[u] = mix_pool.tile([P, HALF_CHUNKS, P], F32, name="first")
            if shared(u):
                nc.vector.tensor_tensor(out=first[u][:], in0=gate_rows[u][:], in1=held, op=ALU.mult)
            else:
                nc.vector.scalar_tensor_tensor(
                    out=first[u][:], in0=beside_rows[u][:], scalar=sig_zeta[:, 0:1], in1=held,
                    op0=ALU.mult, op1=ALU.subtract,
                )

        def mix_gate(u):
            if not shared(u):
                gated[u] = mix_pool.tile([P, HALF_CHUNKS, P], F32, name="gated")
                nc.vector.tensor_tensor(out=gated[u][:], in0=gate_rows[u][:], in1=first[u][:], op=ALU.mult)

        def mix_out(u):
            half, t = divmod(u, HIDDEN_TILES)
            alone = u >= UNITS - STORE_TILES
            width = 1 if alone else STORE_TILES
            member = t % width
            if member == 0:
                out_tiles[u - member] = out_pool.tile([P, HALF_CHUNKS, width * P], F32, name="out_tile")
            out_tile = out_tiles[u - member]
            cols = slice(member * P, (member + 1) * P)
            pieces = 2 if u == UNITS - 1 else 1
            for n in range(pieces):
                part = slice(n * HALF_CHUNKS // pieces, (n + 1) * HALF_CHUNKS // pieces)
                if shared(u):
                    nc.vector.tensor_tensor(
                        out=out_tile[:, part, cols], in0=beside_rows[u][:, part, :], in1=first[u][:, part, :],
                        op=ALU.add,
                    )
                else:
                    nc.vector.scalar_tensor_tensor(
                        out=out_tile[:, part, cols], in0=beside_rows[u][:, part, :], scalar=sig_sum[:, 0:1],
                        in1=gated[u][:, part, :], op0=ALU.mult, op1=ALU.subtract,
                    )
                if member == width - 1:
                    chunks = slice(half * HALF_CHUNKS + part.start, half * HALF_CHUNKS + part.stop)
                    d_cols = slice((t - member) * P, (t + 1) * P)
                    nc.sync.dma_start(out=out_view[:, chunks, d_cols], in_=out_tile[:, part, :])

        vector_copy, scalar_copy = nc.vector.tensor_copy, nc.scalar.copy
        both = list(range(HALF_PAIRS))
        early_acts = [[act_job(0, s, [pair]) for s in range(STREAMS)] for pair in both]
        weight_jobs = [weight_job(g) for g in range(GROUPS)]

        for job, copy in zip(early_acts[0], (vector_copy, scalar_copy)):
            copy_part(job, 0, turn_part(job, 0), copy)
        for s, copy in enumerate((vector_copy, scalar_copy)):
            copy_part(weight_jobs[0], s, turn_part(weight_jobs[0], s), copy)
        bias_turned = banks.tile([P, P], F32, name="bias_turned", tag="bank")
        nc.tensor.transpose(bias_turned[:], bias_rows_f32[:], identity[:])
        bias_cols = keep.tile([P, 2 * HIDDEN_TILES], F32, name="bias_cols")
        nc.scalar.copy(out=bias_cols[:], in_=bias_turned[:, 0 : 2 * HIDDEN_TILES])
        for job in early_acts[0]:
            quantise(job)
        quantise(weight_jobs[0])
        for job, copy in zip(early_acts[1], (vector_copy, scalar_copy)):
            copy_part(job, 0, turn_part(job, 0), copy)
        for u in range(2):
            products(u, [0])
            gates(u, [0])
        for job in early_acts[1]:
            quantise(job)
        copy_part(weight_jobs[1], 0, turn_part(weight_jobs[1], 0), vector_copy)
        for u in range(2):
            products(u, [1])
            gates(u, [1])
        copy_part(weight_jobs[1], 1, turn_part(weight_jobs[1], 1), vector_copy)
        quantise(weight_jobs[1])

        sig_zeta = keep.tile([P, 1], F32, name="sig_zeta")
        sig_nu = keep.tile([P, 1], F32, name="sig_nu")
        nc.scalar.activation(out=sig_zeta[:], in_=zeta_col[:], func=ACT.Sigmoid)
        nc.scalar.activation(out=sig_nu[:], in_=nu_col[:], func=ACT.Sigmoid)
        sig_sum = keep.tile([P, 1], F32, name="sig_sum")
        nc.gpsimd.tensor_tensor(out=sig_sum[:], in0=sig_zeta[:], in1=sig_nu[:], op=ALU.add)
        neg_zeta = keep.tile([P, 1], F32, name="neg_zeta")
        nc.gpsimd.tensor_scalar(out=neg_zeta[:], in0=sig_zeta[:], scalar1=-1.0, scalar2=None, op0=ALU.mult)

        for g in range(2, HEAD_GROUPS):
            copy_part(weight_jobs[g], 0, turn_part(weight_jobs[g], 0), vector_copy)
            copy_part(weight_jobs[g], 1, turn_part(weight_jobs[g], 1), scalar_copy)
            quantise(weight_jobs[g])
        for u in range(2, AHEAD):
            products(u, both)
            gates(u, both)
            if shared(u):
                share(u)

        jobs = weight_jobs[HEAD_GROUPS:] + [act_job(1, s, both) for s in range(STREAMS)]
        jobs_at = {}
        for n, job in enumerate(jobs):
            jobs_at.setdefault(n, []).append(job)

        for v in range(0, UNITS + STEP, STEP):
            for u in range(v + AHEAD, min(v + AHEAD + STEP, UNITS)):
                products(u, both)
                gates(u, both)
                if shared(u):
                    share(u)
            for u in range(v, min(v + STEP, UNITS)):
                turn_back(u)
            for u in range(v, min(v + STEP, UNITS)):
                for job in jobs_at.get(u, []):
                    for part in range(len(job["raws"])):
                        copy_part(job, part, turn_part(job, part), scalar_copy)
            for u in range(v, v + STEP):
                if u < UNITS:
                    mix_first(u)
                if 0 < u <= UNITS:
                    mix_out(u - 1)
                if u < UNITS:
                    mix_gate(u)
                for job in jobs_at.get(u - 1, []):
                    quantise(job)
